import numpy as np
import ml_dtypes


def mxq(x, axis, fmt="e4m3"):
    dtype, down = {"e4m3": (ml_dtypes.float8_e4m3fn, 7), "e5m2": (ml_dtypes.float8_e5m2, 14)}[fmt]
    v = np.moveaxis(np.asarray(x, np.float32).astype(ml_dtypes.bfloat16).astype(np.float64), axis, -1)
    blocks = v.reshape(v.shape[:-1] + (-1, 32))
    amax = np.abs(blocks).max(-1, keepdims=True)
    byte = np.maximum(np.where(amax > 0, np.frexp(amax)[1] - 1 + 127, 0) - down, 1)
    scale = np.exp2(byte - 127.0)
    codes = (blocks / scale).astype(np.float32).astype(dtype).astype(np.float64)
    return np.moveaxis((codes * scale).reshape(v.shape), -1, axis)


WIDE = False


def mx_kscale(k):
    if not WIDE:
        return np.ones(k)
    levels = np.array([10, -10, 5, -5, 0])
    a = np.random.permutation(np.resize(levels, k // 512 * 4)).reshape(k // 512, 4)
    idx = np.arange(k)
    return np.exp2(a[idx // 512, idx % 128 // 32])


BF16 = ml_dtypes.bfloat16


def bf(x):
    return np.asarray(x, np.float32).astype(BF16)


def f64(x):
    return np.asarray(x).astype(np.float64)


T, B, NJ, D, E, HD, R = 128, 4, 16, 1024, 512, 128, 128
BJ = B * NJ
SCALING = 2.0


def setup_inputs():
    s = mx_kscale(D)
    return {"query": bf(np.random.standard_normal((T, BJ, D)) * s),
            "m": bf(np.random.standard_normal((B, T, D)) * s),
            "w_q": bf(np.random.standard_normal((E, D)) * 0.8 / np.sqrt(D) / s),
            "b_q": bf(np.random.standard_normal(E) * 0.2),
            "A_q": bf(np.random.standard_normal((R, D)) / np.sqrt(D) / s),
            "B_q": bf(np.random.standard_normal((E, R)) * 0.3 / np.sqrt(R))}


def reference(query, m, w_q, b_q, A_q, B_q):
    m_exp = np.broadcast_to(f64(m).transpose(1, 0, 2)[:, :, None, :], (T, B, NJ, D)).reshape(T, BJ, D)
    q_in = f64(query) + m_exp
    wq_eff = f64(w_q) + (f64(B_q) @ f64(A_q)) * SCALING
    return (mxq(q_in, 2, "e4m3") @ mxq(wq_eff, 1, "e4m3").T) + f64(b_q)

@@ -1,0 +1,211 @@
+from contextlib import ExitStack
+
+import concourse.mybir as mybir
+from concourse.masks import make_identity
+
+BF16 = mybir.dt.bfloat16
+F32 = mybir.dt.float32
+U32 = mybir.dt.uint32
+U8 = mybir.dt.uint8
+FP8X4 = mybir.dt.float8_e4m3fn_x4
+ADD = mybir.AluOpType.add
+
+P = 128
+FRAMES = 128
+BATCH = 4
+JOINTS = 16
+ROWS = BATCH * JOINTS
+FEATURES = 1024
+OUTPUTS = 512
+RANK = 128
+LORA_SCALE = 2.0
+
+PACK = 4
+PASSES = FEATURES // (P * PACK)
+WORDS = FEATURES // 2
+HALVES = 2
+COLUMN_TILES = OUTPUTS // P
+
+CHUNK = 4
+N_CHUNKS = ROWS // CHUNK
+
+FLOPS = 2 * FRAMES * ROWS * FEATURES * OUTPUTS + 2 * OUTPUTS * RANK * FEATURES
+
+
+def turn_rows(nc, bank, row_words, identity):
+    for u in range(HALVES):
+        for g in range(PASSES):
+            nc.tensor.transpose(
+                bank[:, (u * PASSES + g) * P : (u * PASSES + g + 1) * P],
+                row_words[:, (g * HALVES + u) * P : (g * HALVES + u + 1) * P],
+                identity,
+            )
+
+
+def tile_inversiontemporalmha_pa_t_kernel(tc, query, m, w_q, b_q, A_q, B_q, out):
+    nc = tc.nc
+    with ExitStack() as stack:
+        keep = stack.enter_context(tc.tile_pool(name="keep", bufs=1))
+        q_pool = stack.enter_context(tc.tile_pool(name="q", bufs=N_CHUNKS))
+        grouped_pool = stack.enter_context(tc.tile_pool(name="grouped", bufs=2))
+        packed_pool = stack.enter_context(tc.tile_pool(name="packed", bufs=2))
+        result_pool = stack.enter_context(tc.tile_pool(name="result", bufs=3))
+        turn_psum = stack.enter_context(tc.psum_pool(name="turn_psum", bufs=CHUNK))
+        sum_psum = stack.enter_context(tc.psum_pool(name="sum_psum", bufs=CHUNK))
+
+        m_rows = keep.tile([P, BATCH, FEATURES], BF16)
+        nc.sync.dma_start(out=m_rows[:], in_=m.rearrange("b t k -> t b k"))
+        q_chunks = []
+        for c in range(N_CHUNKS):
+            q_rows = q_pool.tile([P, CHUNK, FEATURES], BF16)
+            q_chunks.append(q_rows)
+        nc.sync.dma_start(out=q_chunks[0][:], in_=query[:, 0:CHUNK, :])
+        b_rows = keep.tile([P, COLUMN_TILES, RANK], BF16)
+        nc.sync.dma_start(out=b_rows[:], in_=B_q.rearrange("(h e) r -> e h r", e=P))
+        a_rows = keep.tile([P, FEATURES], BF16)
+        nc.sync.dma_start(out=a_rows[:], in_=A_q)
+        w_rows = keep.tile([P, COLUMN_TILES, FEATURES], BF16)
+        nc.sync.dma_start(out=w_rows[:], in_=w_q.rearrange("(h e) k -> e h k", e=P))
+        bias_row = keep.tile([P, OUTPUTS], BF16)
+        nc.vector.memset(bias_row[:], 0.0)
+        nc.sync.dma_start(out=bias_row[0:1, :], in_=b_q.rearrange("(o e) -> o e", o=1))
+        for c in range(1, N_CHUNKS):
+            nc.sync.dma_start(
+                out=q_chunks[c][:], in_=query[:, c * CHUNK : (c + 1) * CHUNK, :]
+            )
+
+        identity_f32 = keep.tile([P, P], F32)
+        make_identity(nc, identity_f32[:])
+        identity_bf16 = keep.tile([P, P], BF16)
+        make_identity(nc, identity_bf16[:])
+        ones = keep.tile([P, P], BF16)
+        nc.vector.memset(ones[:], 1.0)
+
+        m_turned = keep.tile([P, BATCH, WORDS], F32)
+        for b in range(BATCH):
+            bank = turn_psum.tile([P, WORDS], F32, tag="turn")
+            turn_rows(nc, bank, m_rows[:, b, :].bitcast(F32), identity_f32[:])
+            nc.scalar.copy(
+                out=m_turned[:, b, :].rearrange("p (x u) -> p x u", u=HALVES),
+                in_=bank[:].rearrange("p (u x) -> p x u", u=HALVES),
+            )
+
+        def turn(c):
+            banks = []
+            for i in range(CHUNK):
+                bank = turn_psum.tile([P, WORDS], F32, tag="turn")
+                turn_rows(nc, bank, q_chunks[c][:, i, :].bitcast(F32), identity_f32[:])
+                banks.append(bank)
+            return banks
+
+        def add_motion(c, banks):
+            b = (c * CHUNK) // JOINTS
+            grouped = grouped_pool.tile([P, CHUNK, FEATURES], BF16, align_bytes=64)
+            for i in range(CHUNK):
+                nc.vector.tensor_tensor(
+                    out=grouped[:, i, :].rearrange("p (x u e) -> p x u e", u=HALVES, e=2),
+                    in0=banks[i][:].bitcast(BF16).rearrange("p (u x e) -> p x u e", u=HALVES, e=2),
+                    in1=m_turned[:, b, :].bitcast(BF16).rearrange("p (x u e) -> p x u e", u=HALVES, e=2),
+                    op=ADD,
+                )
+            return grouped
+
+        def quantise(grouped):
+            codes = packed_pool.tile([P, CHUNK * PASSES * FRAMES], U32, align_bytes=64)
+            scales = packed_pool.tile([P, CHUNK * PASSES * FRAMES], U8, align_bytes=64)
+            nc.vector.quantize_mx(
+                out=codes[:].bitcast(FP8X4),
+                scales=scales[:],
+                in_=grouped[:].rearrange("p i n -> p (i n)"),
+            )
+            return codes, scales
+
+        def multiply(codes, scales):
+            sums = []
+            for i in range(CHUNK):
+                acc = sum_psum.tile([P, OUTPUTS], F32, tag="sum")
+                for g in range(PASSES):
+                    frames = slice((i * PASSES + g) * FRAMES, (i * PASSES + g + 1) * FRAMES)
+                    outputs = slice(g * OUTPUTS, (g + 1) * OUTPUTS)
+                    nc.tensor.matmul_mx(
+                        out=acc[:],
+                        lhsT=codes[:, frames].bitcast(FP8X4),
+                        lhsT_scale=scales[:, frames],
+                        rhs=w_codes[:, outputs].bitcast(FP8X4),
+                        rhs_scale=w_scales[:, outputs],
+                        start=(g == 0),
+                        stop=(g == PASSES - 1),
+                    )
+                sums.append(acc)
+            return sums
+
+        def finish(c, sums):
+            result = result_pool.tile([P, CHUNK, OUTPUTS], F32)
+            for i in range(CHUNK):
+                nc.vector.tensor_tensor(out=result[:, i, :], in0=sums[i][:], in1=bias[:], op=ADD)
+            nc.sync.dma_start(out=out[:, c * CHUNK : (c + 1) * CHUNK, :], in_=result[:])
+
+        banks = turn(0)
+        grouped = add_motion(0, banks)
+        q_codes, q_scales = quantise(grouped)
+
+        b_turned_psum = turn_psum.tile([P, OUTPUTS], BF16, tag="turn")
+        for h in range(COLUMN_TILES):
+            nc.tensor.transpose(
+                b_turned_psum[:, h * P : (h + 1) * P], b_rows[:, h, :], identity_bf16[:]
+            )
+        b_turned = keep.tile([P, OUTPUTS], BF16)
+        nc.scalar.mul(out=b_turned[:], in_=b_turned_psum[:], mul=LORA_SCALE)
+
+        w_grouped = keep.tile([P, PASSES, OUTPUTS, PACK], BF16, align_bytes=64)
+        w_codes = keep.tile([P, PASSES * OUTPUTS], U32, align_bytes=64)
+        w_scales = keep.tile([P, PASSES * OUTPUTS], U8, align_bytes=64)
+        feature_order = "r (g u p e) -> r g u e p"
+        a_by_word = a_rows[:].rearrange(feature_order, g=PASSES, u=HALVES, e=2)
+        for g in range(PASSES):
+            for h in range(COLUMN_TILES):
+                w_by_word = w_rows[:, h, :].rearrange(feature_order, g=PASSES, u=HALVES, e=2)
+                w_turned = sum_psum.tile([P, PACK * P], F32, tag="sum")
+                for u in range(HALVES):
+                    for e in range(2):
+                        plane = w_turned[:, (2 * u + e) * P : (2 * u + e + 1) * P]
+                        nc.tensor.matmul(
+                            out=plane,
+                            lhsT=a_by_word[:, g, u, e, :],
+                            rhs=b_turned[:, h * P : (h + 1) * P],
+                            start=True,
+                            stop=False,
+                        )
+                        nc.tensor.matmul(
+                            out=plane,
+                            lhsT=w_by_word[:, g, u, e, :],
+                            rhs=identity_bf16[:],
+                            start=False,
+                            stop=True,
+                        )
+                nc.scalar.copy(
+                    out=w_grouped[:, g, h * P : (h + 1) * P, :],
+                    in_=w_turned[:].rearrange("p (j e) -> p e j", j=PACK),
+                )
+            outputs = slice(g * OUTPUTS, (g + 1) * OUTPUTS)
+            nc.vector.quantize_mx(
+                out=w_codes[:, outputs].bitcast(FP8X4),
+                scales=w_scales[:, outputs],
+                in_=w_grouped[:, g, :, :].rearrange("p e j -> p (e j)"),
+            )
+
+        bias_psum = sum_psum.tile([P, OUTPUTS], F32, tag="sum")
+        nc.tensor.matmul(out=bias_psum[:], lhsT=ones[:], rhs=bias_row[:], start=True, stop=True)
+        bias = keep.tile([P, OUTPUTS], F32)
+        nc.scalar.copy(out=bias[:], in_=bias_psum[:])
+
+        for c in range(N_CHUNKS):
+            more = c + 1 < N_CHUNKS
+            if more:
+                banks = turn(c + 1)
+            sums = multiply(q_codes, q_scales)
+            if more:
+                grouped = add_motion(c + 1, banks)
+            finish(c, sums)
+            if more:
+                q_codes, q_scales = quantise(grouped)

@@ -28,6 +28,7 @@ COLUMN_TILES = OUTPUTS // P
 
 CHUNK = 4
 N_CHUNKS = ROWS // CHUNK
+DETOUR = 2
 
 FLOPS = 2 * FRAMES * ROWS * FEATURES * OUTPUTS + 2 * OUTPUTS * RANK * FEATURES
 
@@ -141,7 +142,15 @@ def tile_inversiontemporalmha_pa_t_kernel(tc, query, m, w_q, b_q, A_q, B_q, out)
 
         def finish(c, sums):
             result = result_pool.tile([P, CHUNK, OUTPUTS], F32)
-            for i in range(CHUNK):
+            for i in range(DETOUR):
+                nc.scalar.copy(out=result[:, i, :], in_=sums[i][:])
+            nc.gpsimd.tensor_tensor(
+                out=result[:, 0:DETOUR, :],
+                in0=result[:, 0:DETOUR, :],
+                in1=bias[:].unsqueeze(1).to_broadcast([P, DETOUR, OUTPUTS]),
+                op=ADD,
+            )
+            for i in range(DETOUR, CHUNK):
                 nc.vector.tensor_tensor(out=result[:, i, :], in0=sums[i][:], in1=bias[:], op=ADD)
             nc.sync.dma_start(out=out[:, c * CHUNK : (c + 1) * CHUNK, :], in_=result[:])
 

@@ -28,7 +28,8 @@ COLUMN_TILES = OUTPUTS // P
 
 CHUNK = 4
 N_CHUNKS = ROWS // CHUNK
-DETOUR = 2
+CHUNKS_PER_BATCH = JOINTS // CHUNK
+LEAD = 2
 
 FLOPS = 2 * FRAMES * ROWS * FEATURES * OUTPUTS + 2 * OUTPUTS * RANK * FEATURES
 
@@ -49,18 +50,27 @@ def tile_inversiontemporalmha_pa_t_kernel(tc, query, m, w_q, b_q, A_q, B_q, out)
         keep = stack.enter_context(tc.tile_pool(name="keep", bufs=1))
         q_pool = stack.enter_context(tc.tile_pool(name="q", bufs=N_CHUNKS))
         grouped_pool = stack.enter_context(tc.tile_pool(name="grouped", bufs=2))
-        packed_pool = stack.enter_context(tc.tile_pool(name="packed", bufs=2))
+        packed_pool = stack.enter_context(tc.tile_pool(name="packed", bufs=LEAD + 1))
         result_pool = stack.enter_context(tc.tile_pool(name="result", bufs=3))
         turn_psum = stack.enter_context(tc.psum_pool(name="turn_psum", bufs=CHUNK))
         sum_psum = stack.enter_context(tc.psum_pool(name="sum_psum", bufs=CHUNK))
 
+        def load_motion(b):
+            nc.sync.dma_start(out=m_rows[:, b, :], in_=m[b, :, :])
+
+        def load_query(c):
+            nc.sync.dma_start(
+                out=q_chunks[c][:], in_=query[:, c * CHUNK : (c + 1) * CHUNK, :]
+            )
+
         m_rows = keep.tile([P, BATCH, FEATURES], BF16)
-        nc.sync.dma_start(out=m_rows[:], in_=m.rearrange("b t k -> t b k"))
         q_chunks = []
         for c in range(N_CHUNKS):
             q_rows = q_pool.tile([P, CHUNK, FEATURES], BF16)
             q_chunks.append(q_rows)
-        nc.sync.dma_start(out=q_chunks[0][:], in_=query[:, 0:CHUNK, :])
+        load_motion(0)
+        for c in range(LEAD):
+            load_query(c)
         b_rows = keep.tile([P, COLUMN_TILES, RANK], BF16)
         nc.sync.dma_start(out=b_rows[:], in_=B_q.rearrange("(h e) r -> e h r", e=P))
         a_rows = keep.tile([P, FEATURES], BF16)
@@ -70,10 +80,11 @@ def tile_inversiontemporalmha_pa_t_kernel(tc, query, m, w_q, b_q, A_q, B_q, out)
         bias_row = keep.tile([P, OUTPUTS], BF16)
         nc.vector.memset(bias_row[:], 0.0)
         nc.sync.dma_start(out=bias_row[0:1, :], in_=b_q.rearrange("(o e) -> o e", o=1))
-        for c in range(1, N_CHUNKS):
-            nc.sync.dma_start(
-                out=q_chunks[c][:], in_=query[:, c * CHUNK : (c + 1) * CHUNK, :]
-            )
+        load_query(LEAD)
+        for b in range(1, BATCH):
+            load_motion(b)
+        for c in range(LEAD + 1, N_CHUNKS):
+            load_query(c)
 
         identity_f32 = keep.tile([P, P], F32)
         make_identity(nc, identity_f32[:])
@@ -83,7 +94,8 @@ def tile_inversiontemporalmha_pa_t_kernel(tc, query, m, w_q, b_q, A_q, B_q, out)
         nc.vector.memset(ones[:], 1.0)
 
         m_turned = keep.tile([P, BATCH, WORDS], F32)
-        for b in range(BATCH):
+
+        def turn_motion(b):
             bank = turn_psum.tile([P, WORDS], F32, tag="turn")
             turn_rows(nc, bank, m_rows[:, b, :].bitcast(F32), identity_f32[:])
             nc.scalar.copy(
@@ -100,7 +112,7 @@ def tile_inversiontemporalmha_pa_t_kernel(tc, query, m, w_q, b_q, A_q, B_q, out)
             return banks
 
         def add_motion(c, banks):
-            b = (c * CHUNK) // JOINTS
+            b = c // CHUNKS_PER_BATCH
             grouped = grouped_pool.tile([P, CHUNK, FEATURES], BF16, align_bytes=64)
             for i in range(CHUNK):
                 nc.vector.tensor_tensor(
@@ -142,21 +154,20 @@ def tile_inversiontemporalmha_pa_t_kernel(tc, query, m, w_q, b_q, A_q, B_q, out)
 
         def finish(c, sums):
             result = result_pool.tile([P, CHUNK, OUTPUTS], F32)
-            for i in range(DETOUR):
-                nc.scalar.copy(out=result[:, i, :], in_=sums[i][:])
-            nc.gpsimd.tensor_tensor(
-                out=result[:, 0:DETOUR, :],
-                in0=result[:, 0:DETOUR, :],
-                in1=bias[:].unsqueeze(1).to_broadcast([P, DETOUR, OUTPUTS]),
-                op=ADD,
-            )
-            for i in range(DETOUR, CHUNK):
+            step = 1 if c == N_CHUNKS - 1 else CHUNK
+            for i in range(CHUNK):
                 nc.vector.tensor_tensor(out=result[:, i, :], in0=sums[i][:], in1=bias[:], op=ADD)
-            nc.sync.dma_start(out=out[:, c * CHUNK : (c + 1) * CHUNK, :], in_=result[:])
+                if (i + 1) % step == 0:
+                    done = slice(i + 1 - step, i + 1)
+                    nc.sync.dma_start(
+                        out=out[:, c * CHUNK + i + 1 - step : c * CHUNK + i + 1, :],
+                        in_=result[:, done, :],
+                    )
 
-        banks = turn(0)
-        grouped = add_motion(0, banks)
-        q_codes, q_scales = quantise(grouped)
+        turn_motion(0)
+        packed = []
+        for c in range(LEAD):
+            packed.append(quantise(add_motion(c, turn(c))))
 
         b_turned_psum = turn_psum.tile([P, OUTPUTS], BF16, tag="turn")
         for h in range(COLUMN_TILES):
@@ -208,13 +219,16 @@ def tile_inversiontemporalmha_pa_t_kernel(tc, query, m, w_q, b_q, A_q, B_q, out)
         bias = keep.tile([P, OUTPUTS], F32)
         nc.scalar.copy(out=bias[:], in_=bias_psum[:])
 
+        for b in range(1, BATCH):
+            turn_motion(b)
+
         for c in range(N_CHUNKS):
-            more = c + 1 < N_CHUNKS
-            if more:
-                banks = turn(c + 1)
-            sums = multiply(q_codes, q_scales)
-            if more:
-                grouped = add_motion(c + 1, banks)
+            ahead = c + LEAD
+            if ahead < N_CHUNKS:
+                banks = turn(ahead)
+            sums = multiply(packed[c][0], packed[c][1])
+            if ahead < N_CHUNKS:
+                grouped = add_motion(ahead, banks)
             finish(c, sums)
-            if more:
-                q_codes, q_scales = quantise(grouped)
+            if ahead < N_CHUNKS:
+                packed.append(quantise(grouped))

@@ -9,6 +9,7 @@ U32 = mybir.dt.uint32
 U8 = mybir.dt.uint8
 FP8X4 = mybir.dt.float8_e4m3fn_x4
 ADD = mybir.AluOpType.add
+IDENTITY = mybir.ActivationFunctionType.Identity
 
 P = 128
 FRAMES = 128
@@ -29,6 +30,7 @@ COLUMN_TILES = OUTPUTS // P
 CHUNK = 4
 N_CHUNKS = ROWS // CHUNK
 CHUNKS_PER_BATCH = JOINTS // CHUNK
+PAIR = CHUNK // 2
 LEAD = 2
 
 FLOPS = 2 * FRAMES * ROWS * FEATURES * OUTPUTS + 2 * OUTPUTS * RANK * FEATURES
@@ -51,57 +53,19 @@ def tile_inversiontemporalmha_pa_t_kernel(tc, query, m, w_q, b_q, A_q, B_q, out)
         q_pool = stack.enter_context(tc.tile_pool(name="q", bufs=N_CHUNKS))
         grouped_pool = stack.enter_context(tc.tile_pool(name="grouped", bufs=2))
         packed_pool = stack.enter_context(tc.tile_pool(name="packed", bufs=LEAD + 1))
-        result_pool = stack.enter_context(tc.tile_pool(name="result", bufs=3))
         turn_psum = stack.enter_context(tc.psum_pool(name="turn_psum", bufs=CHUNK))
         sum_psum = stack.enter_context(tc.psum_pool(name="sum_psum", bufs=CHUNK))
 
-        def load_motion(b):
-            nc.sync.dma_start(out=m_rows[:, b, :], in_=m[b, :, :])
-
-        def load_query(c):
-            nc.sync.dma_start(
-                out=q_chunks[c][:], in_=query[:, c * CHUNK : (c + 1) * CHUNK, :]
-            )
-
-        m_rows = keep.tile([P, BATCH, FEATURES], BF16)
+        identity_f32 = keep.tile([P, P], F32)
+        m_turned = keep.tile([P, BATCH, WORDS], F32)
+        w_codes = keep.tile([P, PASSES * OUTPUTS], U32, align_bytes=64)
+        w_scales = keep.tile([P, PASSES * OUTPUTS], U8, align_bytes=64)
+        bias_along_free = keep.tile([P, OUTPUTS], F32)
+        bias_by_partition = keep.tile([P, COLUMN_TILES], F32)
         q_chunks = []
         for c in range(N_CHUNKS):
             q_rows = q_pool.tile([P, CHUNK, FEATURES], BF16)
             q_chunks.append(q_rows)
-        load_motion(0)
-        for c in range(LEAD):
-            load_query(c)
-        b_rows = keep.tile([P, COLUMN_TILES, RANK], BF16)
-        nc.sync.dma_start(out=b_rows[:], in_=B_q.rearrange("(h e) r -> e h r", e=P))
-        a_rows = keep.tile([P, FEATURES], BF16)
-        nc.sync.dma_start(out=a_rows[:], in_=A_q)
-        w_rows = keep.tile([P, COLUMN_TILES, FEATURES], BF16)
-        nc.sync.dma_start(out=w_rows[:], in_=w_q.rearrange("(h e) k -> e h k", e=P))
-        bias_row = keep.tile([P, OUTPUTS], BF16)
-        nc.vector.memset(bias_row[:], 0.0)
-        nc.sync.dma_start(out=bias_row[0:1, :], in_=b_q.rearrange("(o e) -> o e", o=1))
-        load_query(LEAD)
-        for b in range(1, BATCH):
-            load_motion(b)
-        for c in range(LEAD + 1, N_CHUNKS):
-            load_query(c)
-
-        identity_f32 = keep.tile([P, P], F32)
-        make_identity(nc, identity_f32[:])
-        identity_bf16 = keep.tile([P, P], BF16)
-        make_identity(nc, identity_bf16[:])
-        ones = keep.tile([P, P], BF16)
-        nc.vector.memset(ones[:], 1.0)
-
-        m_turned = keep.tile([P, BATCH, WORDS], F32)
-
-        def turn_motion(b):
-            bank = turn_psum.tile([P, WORDS], F32, tag="turn")
-            turn_rows(nc, bank, m_rows[:, b, :].bitcast(F32), identity_f32[:])
-            nc.scalar.copy(
-                out=m_turned[:, b, :].rearrange("p (x u) -> p x u", u=HALVES),
-                in_=bank[:].rearrange("p (u x) -> p x u", u=HALVES),
-            )
 
         def turn(c):
             banks = []
@@ -133,17 +97,137 @@ def tile_inversiontemporalmha_pa_t_kernel(tc, query, m, w_q, b_q, A_q, B_q, out)
             )
             return codes, scales
 
-        def multiply(codes, scales):
+        packed = []
+
+        with tc.tile_pool(name="build", bufs=1) as build:
+            def load_motion(b):
+                nc.sync.dma_start(out=m_rows[:, b, :], in_=m[b, :, :])
+
+            def load_query(c):
+                nc.sync.dma_start(
+                    out=q_chunks[c][:], in_=query[:, c * CHUNK : (c + 1) * CHUNK, :]
+                )
+
+            m_rows = build.tile([P, BATCH, FEATURES], BF16)
+            load_motion(0)
+            for c in range(LEAD):
+                load_query(c)
+            b_rows = build.tile([P, COLUMN_TILES, RANK], BF16)
+            nc.sync.dma_start(out=b_rows[:], in_=B_q.rearrange("(h e) r -> e h r", e=P))
+            a_rows = build.tile([P, FEATURES], BF16)
+            nc.sync.dma_start(out=a_rows[:], in_=A_q)
+            w_rows = build.tile([P, COLUMN_TILES, FEATURES], BF16)
+            nc.sync.dma_start(out=w_rows[:], in_=w_q.rearrange("(h e) k -> e h k", e=P))
+            bias_row = build.tile([P, OUTPUTS], BF16)
+            nc.vector.memset(bias_row[:], 0.0)
+            nc.sync.dma_start(out=bias_row[0:1, :], in_=b_q.rearrange("(o e) -> o e", o=1))
+            load_query(LEAD)
+            for b in range(1, BATCH):
+                load_motion(b)
+            for c in range(LEAD + 1, N_CHUNKS):
+                load_query(c)
+
+            make_identity(nc, identity_f32[:])
+            identity_bf16 = build.tile([P, P], BF16)
+            make_identity(nc, identity_bf16[:])
+            ones = build.tile([P, P], BF16)
+            nc.vector.memset(ones[:], 1.0)
+
+            def turn_motion(b):
+                bank = turn_psum.tile([P, WORDS], F32, tag="turn")
+                turn_rows(nc, bank, m_rows[:, b, :].bitcast(F32), identity_f32[:])
+                nc.scalar.copy(
+                    out=m_turned[:, b, :].rearrange("p (x u) -> p x u", u=HALVES),
+                    in_=bank[:].rearrange("p (u x) -> p x u", u=HALVES),
+                )
+
+            turn_motion(0)
+            for c in range(LEAD):
+                packed.append(quantise(add_motion(c, turn(c))))
+
+            b_turned_psum = turn_psum.tile([P, OUTPUTS], BF16, tag="turn")
+            for h in range(COLUMN_TILES):
+                nc.tensor.transpose(
+                    b_turned_psum[:, h * P : (h + 1) * P], b_rows[:, h, :], identity_bf16[:]
+                )
+            b_turned = build.tile([P, OUTPUTS], BF16)
+            nc.scalar.mul(out=b_turned[:], in_=b_turned_psum[:], mul=LORA_SCALE)
+
+            w_grouped = build.tile([P, PASSES, OUTPUTS, PACK], BF16, align_bytes=64)
+            feature_order = "r (g u p e) -> r g u e p"
+            a_by_word = a_rows[:].rearrange(feature_order, g=PASSES, u=HALVES, e=2)
+            for g in range(PASSES):
+                for h in range(COLUMN_TILES):
+                    w_by_word = w_rows[:, h, :].rearrange(feature_order, g=PASSES, u=HALVES, e=2)
+                    w_turned = sum_psum.tile([P, PACK * P], F32, tag="sum")
+                    for u in range(HALVES):
+                        for e in range(2):
+                            plane = w_turned[:, (2 * u + e) * P : (2 * u + e + 1) * P]
+                            nc.tensor.matmul(
+                                out=plane,
+                                lhsT=a_by_word[:, g, u, e, :],
+                                rhs=b_turned[:, h * P : (h + 1) * P],
+                                start=True,
+                                stop=False,
+                            )
+                            nc.tensor.matmul(
+                                out=plane,
+                                lhsT=w_by_word[:, g, u, e, :],
+                                rhs=identity_bf16[:],
+                                start=False,
+                                stop=True,
+                            )
+                    nc.scalar.copy(
+                        out=w_grouped[:, g, h * P : (h + 1) * P, :],
+                        in_=w_turned[:].rearrange("p (j e) -> p e j", j=PACK),
+                    )
+                outputs = slice(g * OUTPUTS, (g + 1) * OUTPUTS)
+                nc.vector.quantize_mx(
+                    out=w_codes[:, outputs].bitcast(FP8X4),
+                    scales=w_scales[:, outputs],
+                    in_=w_grouped[:, g, :, :].rearrange("p e j -> p (e j)"),
+                )
+
+            bias_psum = sum_psum.tile([P, OUTPUTS], F32, tag="sum")
+            nc.tensor.matmul(
+                out=bias_psum[:], lhsT=ones[:], rhs=bias_row[:], start=True, stop=True
+            )
+            nc.scalar.copy(out=bias_along_free[:], in_=bias_psum[:])
+            bias_blocks_psum = sum_psum.tile([P, COLUMN_TILES, P], F32, tag="sum")
+            for h in range(COLUMN_TILES):
+                nc.tensor.matmul(
+                    out=bias_blocks_psum[:, h, :],
+                    lhsT=bias_row[:, h * P : (h + 1) * P],
+                    rhs=ones[:],
+                    start=True,
+                    stop=True,
+                )
+            nc.scalar.copy(out=bias_by_partition[:], in_=bias_blocks_psum[:, :, 0])
+
+            for b in range(1, BATCH):
+                turn_motion(b)
+
+        result_pool = stack.enter_context(tc.tile_pool(name="result", bufs=4))
+        biased_pool = stack.enter_context(tc.tile_pool(name="biased", bufs=2 * PAIR))
+
+        def frame_columns(i, g):
+            return slice((i * PASSES + g) * FRAMES, (i * PASSES + g + 1) * FRAMES)
+
+        def store(c, first, result):
+            bj = c * CHUNK + first
+            nc.sync.dma_start(out=out[:, bj : bj + PAIR, :], in_=result[:])
+
+        def multiply(c, first):
+            codes, scales = packed[c]
             sums = []
-            for i in range(CHUNK):
+            for i in range(first, first + PAIR):
                 acc = sum_psum.tile([P, OUTPUTS], F32, tag="sum")
                 for g in range(PASSES):
-                    frames = slice((i * PASSES + g) * FRAMES, (i * PASSES + g + 1) * FRAMES)
                     outputs = slice(g * OUTPUTS, (g + 1) * OUTPUTS)
                     nc.tensor.matmul_mx(
                         out=acc[:],
-                        lhsT=codes[:, frames].bitcast(FP8X4),
-                        lhsT_scale=scales[:, frames],
+                        lhsT=codes[:, frame_columns(i, g)].bitcast(FP8X4),
+                        lhsT_scale=scales[:, frame_columns(i, g)],
                         rhs=w_codes[:, outputs].bitcast(FP8X4),
                         rhs_scale=w_scales[:, outputs],
                         start=(g == 0),
@@ -152,83 +236,65 @@ def tile_inversiontemporalmha_pa_t_kernel(tc, query, m, w_q, b_q, A_q, B_q, out)
                 sums.append(acc)
             return sums
 
-        def finish(c, sums):
-            result = result_pool.tile([P, CHUNK, OUTPUTS], F32)
-            step = 1 if c == N_CHUNKS - 1 else CHUNK
-            for i in range(CHUNK):
-                nc.vector.tensor_tensor(out=result[:, i, :], in0=sums[i][:], in1=bias[:], op=ADD)
-                if (i + 1) % step == 0:
-                    done = slice(i + 1 - step, i + 1)
-                    nc.sync.dma_start(
-                        out=out[:, c * CHUNK + i + 1 - step : c * CHUNK + i + 1, :],
-                        in_=result[:, done, :],
-                    )
-
-        turn_motion(0)
-        packed = []
-        for c in range(LEAD):
-            packed.append(quantise(add_motion(c, turn(c))))
-
-        b_turned_psum = turn_psum.tile([P, OUTPUTS], BF16, tag="turn")
-        for h in range(COLUMN_TILES):
-            nc.tensor.transpose(
-                b_turned_psum[:, h * P : (h + 1) * P], b_rows[:, h, :], identity_bf16[:]
-            )
-        b_turned = keep.tile([P, OUTPUTS], BF16)
-        nc.scalar.mul(out=b_turned[:], in_=b_turned_psum[:], mul=LORA_SCALE)
-
-        w_grouped = keep.tile([P, PASSES, OUTPUTS, PACK], BF16, align_bytes=64)
-        w_codes = keep.tile([P, PASSES * OUTPUTS], U32, align_bytes=64)
-        w_scales = keep.tile([P, PASSES * OUTPUTS], U8, align_bytes=64)
-        feature_order = "r (g u p e) -> r g u e p"
-        a_by_word = a_rows[:].rearrange(feature_order, g=PASSES, u=HALVES, e=2)
-        for g in range(PASSES):
-            for h in range(COLUMN_TILES):
-                w_by_word = w_rows[:, h, :].rearrange(feature_order, g=PASSES, u=HALVES, e=2)
-                w_turned = sum_psum.tile([P, PACK * P], F32, tag="sum")
-                for u in range(HALVES):
-                    for e in range(2):
-                        plane = w_turned[:, (2 * u + e) * P : (2 * u + e + 1) * P]
-                        nc.tensor.matmul(
-                            out=plane,
-                            lhsT=a_by_word[:, g, u, e, :],
-                            rhs=b_turned[:, h * P : (h + 1) * P],
-                            start=True,
-                            stop=False,
-                        )
-                        nc.tensor.matmul(
-                            out=plane,
-                            lhsT=w_by_word[:, g, u, e, :],
-                            rhs=identity_bf16[:],
-                            start=False,
-                            stop=True,
-                        )
-                nc.scalar.copy(
-                    out=w_grouped[:, g, h * P : (h + 1) * P, :],
-                    in_=w_turned[:].rearrange("p (j e) -> p e j", j=PACK),
+        def add_bias_and_store(c, first, sums):
+            result = result_pool.tile([P, PAIR, OUTPUTS], F32)
+            for n in range(PAIR):
+                nc.vector.tensor_tensor(
+                    out=result[:, n, :], in0=sums[n][:], in1=bias_along_free[:], op=ADD
                 )
-            outputs = slice(g * OUTPUTS, (g + 1) * OUTPUTS)
-            nc.vector.quantize_mx(
-                out=w_codes[:, outputs].bitcast(FP8X4),
-                scales=w_scales[:, outputs],
-                in_=w_grouped[:, g, :, :].rearrange("p e j -> p (e j)"),
-            )
+            store(c, first, result)
 
-        bias_psum = sum_psum.tile([P, OUTPUTS], F32, tag="sum")
-        nc.tensor.matmul(out=bias_psum[:], lhsT=ones[:], rhs=bias_row[:], start=True, stop=True)
-        bias = keep.tile([P, OUTPUTS], F32)
-        nc.scalar.copy(out=bias[:], in_=bias_psum[:])
+        def multiply_turned(c, first):
+            codes, scales = packed[c]
+            turned = []
+            for i in range(first, first + PAIR):
+                acc = sum_psum.tile([P, COLUMN_TILES, FRAMES], F32, tag="sum")
+                biased = biased_pool.tile([P, COLUMN_TILES, FRAMES], F32)
+                for h in range(COLUMN_TILES):
+                    for g in range(PASSES):
+                        outputs = slice(g * OUTPUTS + h * P, g * OUTPUTS + (h + 1) * P)
+                        nc.tensor.matmul_mx(
+                            out=acc[:, h, :],
+                            lhsT=w_codes[:, outputs].bitcast(FP8X4),
+                            lhsT_scale=w_scales[:, outputs],
+                            rhs=codes[:, frame_columns(i, g)].bitcast(FP8X4),
+                            rhs_scale=scales[:, frame_columns(i, g)],
+                            start=(g == 0),
+                            stop=(g == PASSES - 1),
+                        )
+                    nc.scalar.activation(
+                        out=biased[:, h, :],
+                        in_=acc[:, h, :],
+                        func=IDENTITY,
+                        bias=bias_by_partition[:, h : h + 1],
+                    )
+                turned.append(biased)
+            return turned
 
-        for b in range(1, BATCH):
-            turn_motion(b)
+        def turn_back_and_store(c, first, turned):
+            result = result_pool.tile([P, PAIR, OUTPUTS], F32)
+            for n in range(PAIR):
+                bank = sum_psum.tile([P, COLUMN_TILES, P], F32, tag="sum")
+                for h in range(COLUMN_TILES):
+                    nc.tensor.transpose(bank[:, h, :], turned[n][:, h, :], identity_f32[:])
+                nc.scalar.copy(out=result[:, n, :], in_=bank[:].rearrange("p h e -> p (h e)"))
+            store(c, first, result)
 
+        turned = []
         for c in range(N_CHUNKS):
             ahead = c + LEAD
-            if ahead < N_CHUNKS:
+            preparing = ahead < N_CHUNKS
+            if preparing:
                 banks = turn(ahead)
-            sums = multiply(packed[c][0], packed[c][1])
-            if ahead < N_CHUNKS:
+            if turned:
+                turn_back_and_store(c - 1, PAIR, turned)
+            sums = multiply(c, 0)
+            if preparing:
+                turned = multiply_turned(c, PAIR)
                 grouped = add_motion(ahead, banks)
-            finish(c, sums)
-            if ahead < N_CHUNKS:
+                add_bias_and_store(c, 0, sums)
                 packed.append(quantise(grouped))
+            else:
+                turned = []
+                add_bias_and_store(c, 0, sums)
+                add_bias_and_store(c, PAIR, multiply(c, PAIR))

@@ -30,7 +30,8 @@ COLUMN_TILES = OUTPUTS // P
 CHUNK = 4
 N_CHUNKS = ROWS // CHUNK
 CHUNKS_PER_BATCH = JOINTS // CHUNK
-PAIR = CHUNK // 2
+TURNED = 1
+DIRECT = CHUNK - TURNED
 LEAD = 2
 
 FLOPS = 2 * FRAMES * ROWS * FEATURES * OUTPUTS + 2 * OUTPUTS * RANK * FEATURES
@@ -208,19 +209,19 @@ def tile_inversiontemporalmha_pa_t_kernel(tc, query, m, w_q, b_q, A_q, B_q, out)
                 turn_motion(b)
 
         result_pool = stack.enter_context(tc.tile_pool(name="result", bufs=4))
-        biased_pool = stack.enter_context(tc.tile_pool(name="biased", bufs=2 * PAIR))
+        biased_pool = stack.enter_context(tc.tile_pool(name="biased", bufs=2 * TURNED))
 
         def frame_columns(i, g):
             return slice((i * PASSES + g) * FRAMES, (i * PASSES + g + 1) * FRAMES)
 
-        def store(c, first, result):
+        def store(c, first, count, result):
             bj = c * CHUNK + first
-            nc.sync.dma_start(out=out[:, bj : bj + PAIR, :], in_=result[:])
+            nc.sync.dma_start(out=out[:, bj : bj + count, :], in_=result[:, 0:count, :])
 
-        def multiply(c, first):
+        def multiply(c, first, count):
             codes, scales = packed[c]
             sums = []
-            for i in range(first, first + PAIR):
+            for i in range(first, first + count):
                 acc = sum_psum.tile([P, OUTPUTS], F32, tag="sum")
                 for g in range(PASSES):
                     outputs = slice(g * OUTPUTS, (g + 1) * OUTPUTS)
@@ -237,17 +238,17 @@ def tile_inversiontemporalmha_pa_t_kernel(tc, query, m, w_q, b_q, A_q, B_q, out)
             return sums
 
         def add_bias_and_store(c, first, sums):
-            result = result_pool.tile([P, PAIR, OUTPUTS], F32)
-            for n in range(PAIR):
+            result = result_pool.tile([P, DIRECT, OUTPUTS], F32)
+            for n in range(len(sums)):
                 nc.vector.tensor_tensor(
                     out=result[:, n, :], in0=sums[n][:], in1=bias_along_free[:], op=ADD
                 )
-            store(c, first, result)
+            store(c, first, len(sums), result)
 
-        def multiply_turned(c, first):
+        def multiply_turned(c, first, count):
             codes, scales = packed[c]
             turned = []
-            for i in range(first, first + PAIR):
+            for i in range(first, first + count):
                 acc = sum_psum.tile([P, COLUMN_TILES, FRAMES], F32, tag="sum")
                 biased = biased_pool.tile([P, COLUMN_TILES, FRAMES], F32)
                 for h in range(COLUMN_TILES):
@@ -272,29 +273,30 @@ def tile_inversiontemporalmha_pa_t_kernel(tc, query, m, w_q, b_q, A_q, B_q, out)
             return turned
 
         def turn_back_and_store(c, first, turned):
-            result = result_pool.tile([P, PAIR, OUTPUTS], F32)
-            for n in range(PAIR):
+            result = result_pool.tile([P, DIRECT, OUTPUTS], F32)
+            for n in range(len(turned)):
                 bank = sum_psum.tile([P, COLUMN_TILES, P], F32, tag="sum")
                 for h in range(COLUMN_TILES):
                     nc.tensor.transpose(bank[:, h, :], turned[n][:, h, :], identity_f32[:])
                 nc.scalar.copy(out=result[:, n, :], in_=bank[:].rearrange("p h e -> p (h e)"))
-            store(c, first, result)
+            store(c, first, len(turned), result)
 
-        turned = []
-        for c in range(N_CHUNKS):
-            ahead = c + LEAD
-            preparing = ahead < N_CHUNKS
-            if preparing:
-                banks = turn(ahead)
-            if turned:
-                turn_back_and_store(c - 1, PAIR, turned)
-            sums = multiply(c, 0)
-            if preparing:
-                turned = multiply_turned(c, PAIR)
-                grouped = add_motion(ahead, banks)
-                add_bias_and_store(c, 0, sums)
-                packed.append(quantise(grouped))
-            else:
-                turned = []
-                add_bias_and_store(c, 0, sums)
-                add_bias_and_store(c, PAIR, multiply(c, PAIR))
+        with tc.manual_schedule():
+            turned = []
+            for c in range(N_CHUNKS):
+                ahead = c + LEAD
+                preparing = ahead < N_CHUNKS
+                if preparing:
+                    banks = turn(ahead)
+                if turned:
+                    turn_back_and_store(c - 1, DIRECT, turned)
+                sums = multiply(c, 0, DIRECT)
+                if preparing:
+                    turned = multiply_turned(c, DIRECT, TURNED)
+                    grouped = add_motion(ahead, banks)
+                    add_bias_and_store(c, 0, sums)
+                    packed.append(quantise(grouped))
+                else:
+                    turned = []
+                    add_bias_and_store(c, 0, sums)
+                    add_bias_and_store(c, DIRECT, multiply(c, DIRECT, TURNED))

@@ -9,7 +9,6 @@ U32 = mybir.dt.uint32
 U8 = mybir.dt.uint8
 FP8X4 = mybir.dt.float8_e4m3fn_x4
 ADD = mybir.AluOpType.add
-IDENTITY = mybir.ActivationFunctionType.Identity
 
 P = 128
 FRAMES = 128
@@ -30,9 +29,8 @@ COLUMN_TILES = OUTPUTS // P
 CHUNK = 4
 N_CHUNKS = ROWS // CHUNK
 CHUNKS_PER_BATCH = JOINTS // CHUNK
-TURNED = 1
-DIRECT = CHUNK - TURNED
 LEAD = 2
+DETOUR = 1
 
 FLOPS = 2 * FRAMES * ROWS * FEATURES * OUTPUTS + 2 * OUTPUTS * RANK * FEATURES
 
@@ -54,19 +52,57 @@ def tile_inversiontemporalmha_pa_t_kernel(tc, query, m, w_q, b_q, A_q, B_q, out)
         q_pool = stack.enter_context(tc.tile_pool(name="q", bufs=N_CHUNKS))
         grouped_pool = stack.enter_context(tc.tile_pool(name="grouped", bufs=2))
         packed_pool = stack.enter_context(tc.tile_pool(name="packed", bufs=LEAD + 1))
+        result_pool = stack.enter_context(tc.tile_pool(name="result", bufs=3))
         turn_psum = stack.enter_context(tc.psum_pool(name="turn_psum", bufs=CHUNK))
         sum_psum = stack.enter_context(tc.psum_pool(name="sum_psum", bufs=CHUNK))
 
-        identity_f32 = keep.tile([P, P], F32)
-        m_turned = keep.tile([P, BATCH, WORDS], F32)
-        w_codes = keep.tile([P, PASSES * OUTPUTS], U32, align_bytes=64)
-        w_scales = keep.tile([P, PASSES * OUTPUTS], U8, align_bytes=64)
-        bias_along_free = keep.tile([P, OUTPUTS], F32)
-        bias_by_partition = keep.tile([P, COLUMN_TILES], F32)
+        def load_motion(b):
+            nc.sync.dma_start(out=m_rows[:, b, :], in_=m[b, :, :])
+
+        def load_query(c):
+            nc.sync.dma_start(
+                out=q_chunks[c][:], in_=query[:, c * CHUNK : (c + 1) * CHUNK, :]
+            )
+
+        m_rows = keep.tile([P, BATCH, FEATURES], BF16)
         q_chunks = []
         for c in range(N_CHUNKS):
             q_rows = q_pool.tile([P, CHUNK, FEATURES], BF16)
             q_chunks.append(q_rows)
+        load_motion(0)
+        for c in range(LEAD):
+            load_query(c)
+        b_rows = keep.tile([P, COLUMN_TILES, RANK], BF16)
+        nc.sync.dma_start(out=b_rows[:], in_=B_q.rearrange("(h e) r -> e h r", e=P))
+        a_rows = keep.tile([P, FEATURES], BF16)
+        nc.sync.dma_start(out=a_rows[:], in_=A_q)
+        w_rows = keep.tile([P, COLUMN_TILES, FEATURES], BF16)
+        nc.sync.dma_start(out=w_rows[:], in_=w_q.rearrange("(h e) k -> e h k", e=P))
+        bias_row = keep.tile([P, OUTPUTS], BF16)
+        nc.vector.memset(bias_row[:], 0.0)
+        nc.sync.dma_start(out=bias_row[0:1, :], in_=b_q.rearrange("(o e) -> o e", o=1))
+        load_query(LEAD)
+        for b in range(1, BATCH):
+            load_motion(b)
+        for c in range(LEAD + 1, N_CHUNKS):
+            load_query(c)
+
+        identity_f32 = keep.tile([P, P], F32)
+        make_identity(nc, identity_f32[:])
+        identity_bf16 = keep.tile([P, P], BF16)
+        make_identity(nc, identity_bf16[:])
+        ones = keep.tile([P, P], BF16)
+        nc.vector.memset(ones[:], 1.0)
+
+        m_turned = keep.tile([P, BATCH, WORDS], F32)
+
+        def turn_motion(b):
+            bank = turn_psum.tile([P, WORDS], F32, tag="turn")
+            turn_rows(nc, bank, m_rows[:, b, :].bitcast(F32), identity_f32[:])
+            nc.scalar.copy(
+                out=m_turned[:, b, :].rearrange("p (x u) -> p x u", u=HALVES),
+                in_=bank[:].rearrange("p (u x) -> p x u", u=HALVES),
+            )
 
         def turn(c):
             banks = []
@@ -98,137 +134,17 @@ def tile_inversiontemporalmha_pa_t_kernel(tc, query, m, w_q, b_q, A_q, B_q, out)
             )
             return codes, scales
 
-        packed = []
-
-        with tc.tile_pool(name="build", bufs=1) as build:
-            def load_motion(b):
-                nc.sync.dma_start(out=m_rows[:, b, :], in_=m[b, :, :])
-
-            def load_query(c):
-                nc.sync.dma_start(
-                    out=q_chunks[c][:], in_=query[:, c * CHUNK : (c + 1) * CHUNK, :]
-                )
-
-            m_rows = build.tile([P, BATCH, FEATURES], BF16)
-            load_motion(0)
-            for c in range(LEAD):
-                load_query(c)
-            b_rows = build.tile([P, COLUMN_TILES, RANK], BF16)
-            nc.sync.dma_start(out=b_rows[:], in_=B_q.rearrange("(h e) r -> e h r", e=P))
-            a_rows = build.tile([P, FEATURES], BF16)
-            nc.sync.dma_start(out=a_rows[:], in_=A_q)
-            w_rows = build.tile([P, COLUMN_TILES, FEATURES], BF16)
-            nc.sync.dma_start(out=w_rows[:], in_=w_q.rearrange("(h e) k -> e h k", e=P))
-            bias_row = build.tile([P, OUTPUTS], BF16)
-            nc.vector.memset(bias_row[:], 0.0)
-            nc.sync.dma_start(out=bias_row[0:1, :], in_=b_q.rearrange("(o e) -> o e", o=1))
-            load_query(LEAD)
-            for b in range(1, BATCH):
-                load_motion(b)
-            for c in range(LEAD + 1, N_CHUNKS):
-                load_query(c)
-
-            make_identity(nc, identity_f32[:])
-            identity_bf16 = build.tile([P, P], BF16)
-            make_identity(nc, identity_bf16[:])
-            ones = build.tile([P, P], BF16)
-            nc.vector.memset(ones[:], 1.0)
-
-            def turn_motion(b):
-                bank = turn_psum.tile([P, WORDS], F32, tag="turn")
-                turn_rows(nc, bank, m_rows[:, b, :].bitcast(F32), identity_f32[:])
-                nc.scalar.copy(
-                    out=m_turned[:, b, :].rearrange("p (x u) -> p x u", u=HALVES),
-                    in_=bank[:].rearrange("p (u x) -> p x u", u=HALVES),
-                )
-
-            turn_motion(0)
-            for c in range(LEAD):
-                packed.append(quantise(add_motion(c, turn(c))))
-
-            b_turned_psum = turn_psum.tile([P, OUTPUTS], BF16, tag="turn")
-            for h in range(COLUMN_TILES):
-                nc.tensor.transpose(
-                    b_turned_psum[:, h * P : (h + 1) * P], b_rows[:, h, :], identity_bf16[:]
-                )
-            b_turned = build.tile([P, OUTPUTS], BF16)
-            nc.scalar.mul(out=b_turned[:], in_=b_turned_psum[:], mul=LORA_SCALE)
-
-            w_grouped = build.tile([P, PASSES, OUTPUTS, PACK], BF16, align_bytes=64)
-            feature_order = "r (g u p e) -> r g u e p"
-            a_by_word = a_rows[:].rearrange(feature_order, g=PASSES, u=HALVES, e=2)
-            for g in range(PASSES):
-                for h in range(COLUMN_TILES):
-                    w_by_word = w_rows[:, h, :].rearrange(feature_order, g=PASSES, u=HALVES, e=2)
-                    w_turned = sum_psum.tile([P, PACK * P], F32, tag="sum")
-                    for u in range(HALVES):
-                        for e in range(2):
-                            plane = w_turned[:, (2 * u + e) * P : (2 * u + e + 1) * P]
-                            nc.tensor.matmul(
-                                out=plane,
-                                lhsT=a_by_word[:, g, u, e, :],
-                                rhs=b_turned[:, h * P : (h + 1) * P],
-                                start=True,
-                                stop=False,
-                            )
-                            nc.tensor.matmul(
-                                out=plane,
-                                lhsT=w_by_word[:, g, u, e, :],
-                                rhs=identity_bf16[:],
-                                start=False,
-                                stop=True,
-                            )
-                    nc.scalar.copy(
-                        out=w_grouped[:, g, h * P : (h + 1) * P, :],
-                        in_=w_turned[:].rearrange("p (j e) -> p e j", j=PACK),
-                    )
-                outputs = slice(g * OUTPUTS, (g + 1) * OUTPUTS)
-                nc.vector.quantize_mx(
-                    out=w_codes[:, outputs].bitcast(FP8X4),
-                    scales=w_scales[:, outputs],
-                    in_=w_grouped[:, g, :, :].rearrange("p e j -> p (e j)"),
-                )
-
-            bias_psum = sum_psum.tile([P, OUTPUTS], F32, tag="sum")
-            nc.tensor.matmul(
-                out=bias_psum[:], lhsT=ones[:], rhs=bias_row[:], start=True, stop=True
-            )
-            nc.scalar.copy(out=bias_along_free[:], in_=bias_psum[:])
-            bias_blocks_psum = sum_psum.tile([P, COLUMN_TILES, P], F32, tag="sum")
-            for h in range(COLUMN_TILES):
-                nc.tensor.matmul(
-                    out=bias_blocks_psum[:, h, :],
-                    lhsT=bias_row[:, h * P : (h + 1) * P],
-                    rhs=ones[:],
-                    start=True,
-                    stop=True,
-                )
-            nc.scalar.copy(out=bias_by_partition[:], in_=bias_blocks_psum[:, :, 0])
-
-            for b in range(1, BATCH):
-                turn_motion(b)
-
-        result_pool = stack.enter_context(tc.tile_pool(name="result", bufs=4))
-        biased_pool = stack.enter_context(tc.tile_pool(name="biased", bufs=2 * TURNED))
-
-        def frame_columns(i, g):
-            return slice((i * PASSES + g) * FRAMES, (i * PASSES + g + 1) * FRAMES)
-
-        def store(c, first, count, result):
-            bj = c * CHUNK + first
-            nc.sync.dma_start(out=out[:, bj : bj + count, :], in_=result[:, 0:count, :])
-
-        def multiply(c, first, count):
-            codes, scales = packed[c]
+        def multiply(codes, scales):
             sums = []
-            for i in range(first, first + count):
+            for i in range(CHUNK):
                 acc = sum_psum.tile([P, OUTPUTS], F32, tag="sum")
                 for g in range(PASSES):
+                    frames = slice((i * PASSES + g) * FRAMES, (i * PASSES + g + 1) * FRAMES)
                     outputs = slice(g * OUTPUTS, (g + 1) * OUTPUTS)
                     nc.tensor.matmul_mx(
                         out=acc[:],
-                        lhsT=codes[:, frame_columns(i, g)].bitcast(FP8X4),
-                        lhsT_scale=scales[:, frame_columns(i, g)],
+                        lhsT=codes[:, frames].bitcast(FP8X4),
+                        lhsT_scale=scales[:, frames],
                         rhs=w_codes[:, outputs].bitcast(FP8X4),
                         rhs_scale=w_scales[:, outputs],
                         start=(g == 0),
@@ -237,66 +153,91 @@ def tile_inversiontemporalmha_pa_t_kernel(tc, query, m, w_q, b_q, A_q, B_q, out)
                 sums.append(acc)
             return sums
 
-        def add_bias_and_store(c, first, sums):
-            result = result_pool.tile([P, DIRECT, OUTPUTS], F32)
-            for n in range(len(sums)):
-                nc.vector.tensor_tensor(
-                    out=result[:, n, :], in0=sums[n][:], in1=bias_along_free[:], op=ADD
-                )
-            store(c, first, len(sums), result)
-
-        def multiply_turned(c, first, count):
-            codes, scales = packed[c]
-            turned = []
-            for i in range(first, first + count):
-                acc = sum_psum.tile([P, COLUMN_TILES, FRAMES], F32, tag="sum")
-                biased = biased_pool.tile([P, COLUMN_TILES, FRAMES], F32)
-                for h in range(COLUMN_TILES):
-                    for g in range(PASSES):
-                        outputs = slice(g * OUTPUTS + h * P, g * OUTPUTS + (h + 1) * P)
-                        nc.tensor.matmul_mx(
-                            out=acc[:, h, :],
-                            lhsT=w_codes[:, outputs].bitcast(FP8X4),
-                            lhsT_scale=w_scales[:, outputs],
-                            rhs=codes[:, frame_columns(i, g)].bitcast(FP8X4),
-                            rhs_scale=scales[:, frame_columns(i, g)],
-                            start=(g == 0),
-                            stop=(g == PASSES - 1),
-                        )
-                    nc.scalar.activation(
-                        out=biased[:, h, :],
-                        in_=acc[:, h, :],
-                        func=IDENTITY,
-                        bias=bias_by_partition[:, h : h + 1],
+        def finish(c, sums):
+            result = result_pool.tile([P, CHUNK, OUTPUTS], F32)
+            step = 1 if c == N_CHUNKS - 1 else CHUNK
+            for i in range(CHUNK):
+                if i < DETOUR:
+                    nc.scalar.copy(out=result[:, i, :], in_=sums[i][:])
+                    nc.gpsimd.tensor_tensor(
+                        out=result[:, i, :], in0=result[:, i, :], in1=bias[:], op=ADD
                     )
-                turned.append(biased)
-            return turned
-
-        def turn_back_and_store(c, first, turned):
-            result = result_pool.tile([P, DIRECT, OUTPUTS], F32)
-            for n in range(len(turned)):
-                bank = sum_psum.tile([P, COLUMN_TILES, P], F32, tag="sum")
-                for h in range(COLUMN_TILES):
-                    nc.tensor.transpose(bank[:, h, :], turned[n][:, h, :], identity_f32[:])
-                nc.scalar.copy(out=result[:, n, :], in_=bank[:].rearrange("p h e -> p (h e)"))
-            store(c, first, len(turned), result)
-
-        with tc.manual_schedule():
-            turned = []
-            for c in range(N_CHUNKS):
-                ahead = c + LEAD
-                preparing = ahead < N_CHUNKS
-                if preparing:
-                    banks = turn(ahead)
-                if turned:
-                    turn_back_and_store(c - 1, DIRECT, turned)
-                sums = multiply(c, 0, DIRECT)
-                if preparing:
-                    turned = multiply_turned(c, DIRECT, TURNED)
-                    grouped = add_motion(ahead, banks)
-                    add_bias_and_store(c, 0, sums)
-                    packed.append(quantise(grouped))
                 else:
-                    turned = []
-                    add_bias_and_store(c, 0, sums)
-                    add_bias_and_store(c, DIRECT, multiply(c, DIRECT, TURNED))
+                    nc.vector.tensor_tensor(
+                        out=result[:, i, :], in0=sums[i][:], in1=bias[:], op=ADD
+                    )
+                if (i + 1) % step == 0:
+                    done = slice(i + 1 - step, i + 1)
+                    nc.sync.dma_start(
+                        out=out[:, c * CHUNK + i + 1 - step : c * CHUNK + i + 1, :],
+                        in_=result[:, done, :],
+                    )
+
+        turn_motion(0)
+        packed = []
+        for c in range(LEAD):
+            packed.append(quantise(add_motion(c, turn(c))))
+
+        b_turned_psum = turn_psum.tile([P, OUTPUTS], BF16, tag="turn")
+        for h in range(COLUMN_TILES):
+            nc.tensor.transpose(
+                b_turned_psum[:, h * P : (h + 1) * P], b_rows[:, h, :], identity_bf16[:]
+            )
+        b_turned = keep.tile([P, OUTPUTS], BF16)
+        nc.scalar.mul(out=b_turned[:], in_=b_turned_psum[:], mul=LORA_SCALE)
+
+        w_grouped = keep.tile([P, PASSES, OUTPUTS, PACK], BF16, align_bytes=64)
+        w_codes = keep.tile([P, PASSES * OUTPUTS], U32, align_bytes=64)
+        w_scales = keep.tile([P, PASSES * OUTPUTS], U8, align_bytes=64)
+        feature_order = "r (g u p e) -> r g u e p"
+        a_by_word = a_rows[:].rearrange(feature_order, g=PASSES, u=HALVES, e=2)
+        for g in range(PASSES):
+            for h in range(COLUMN_TILES):
+                w_by_word = w_rows[:, h, :].rearrange(feature_order, g=PASSES, u=HALVES, e=2)
+                w_turned = sum_psum.tile([P, PACK * P], F32, tag="sum")
+                for u in range(HALVES):
+                    for e in range(2):
+                        plane = w_turned[:, (2 * u + e) * P : (2 * u + e + 1) * P]
+                        nc.tensor.matmul(
+                            out=plane,
+                            lhsT=a_by_word[:, g, u, e, :],
+                            rhs=b_turned[:, h * P : (h + 1) * P],
+                            start=True,
+                            stop=False,
+                        )
+                        nc.tensor.matmul(
+                            out=plane,
+                            lhsT=w_by_word[:, g, u, e, :],
+                            rhs=identity_bf16[:],
+                            start=False,
+                            stop=True,
+                        )
+                nc.scalar.copy(
+                    out=w_grouped[:, g, h * P : (h + 1) * P, :],
+                    in_=w_turned[:].rearrange("p (j e) -> p e j", j=PACK),
+                )
+            outputs = slice(g * OUTPUTS, (g + 1) * OUTPUTS)
+            nc.vector.quantize_mx(
+                out=w_codes[:, outputs].bitcast(FP8X4),
+                scales=w_scales[:, outputs],
+                in_=w_grouped[:, g, :, :].rearrange("p e j -> p (e j)"),
+            )
+
+        bias_psum = sum_psum.tile([P, OUTPUTS], F32, tag="sum")
+        nc.tensor.matmul(out=bias_psum[:], lhsT=ones[:], rhs=bias_row[:], start=True, stop=True)
+        bias = keep.tile([P, OUTPUTS], F32)
+        nc.scalar.copy(out=bias[:], in_=bias_psum[:])
+
+        for b in range(1, BATCH):
+            turn_motion(b)
+
+        for c in range(N_CHUNKS):
+            ahead = c + LEAD
+            if ahead < N_CHUNKS:
+                banks = turn(ahead)
+            sums = multiply(packed[c][0], packed[c][1])
+            if ahead < N_CHUNKS:
+                grouped = add_motion(ahead, banks)
+            finish(c, sums)
+            if ahead < N_CHUNKS:
+                packed.append(quantise(grouped))

@@ -9,6 +9,7 @@ U32 = mybir.dt.uint32
 U8 = mybir.dt.uint8
 FP8X4 = mybir.dt.float8_e4m3fn_x4
 ADD = mybir.AluOpType.add
+IDENTITY = mybir.ActivationFunctionType.Identity
 
 P = 128
 FRAMES = 128
@@ -29,8 +30,10 @@ COLUMN_TILES = OUTPUTS // P
 CHUNK = 4
 N_CHUNKS = ROWS // CHUNK
 CHUNKS_PER_BATCH = JOINTS // CHUNK
-LEAD = 2
+TURNED = 1
+DIRECT = CHUNK - TURNED
 DETOUR = 1
+LEAD = 2
 
 FLOPS = 2 * FRAMES * ROWS * FEATURES * OUTPUTS + 2 * OUTPUTS * RANK * FEATURES
 
@@ -52,57 +55,19 @@ def tile_inversiontemporalmha_pa_t_kernel(tc, query, m, w_q, b_q, A_q, B_q, out)
         q_pool = stack.enter_context(tc.tile_pool(name="q", bufs=N_CHUNKS))
         grouped_pool = stack.enter_context(tc.tile_pool(name="grouped", bufs=2))
         packed_pool = stack.enter_context(tc.tile_pool(name="packed", bufs=LEAD + 1))
-        result_pool = stack.enter_context(tc.tile_pool(name="result", bufs=3))
         turn_psum = stack.enter_context(tc.psum_pool(name="turn_psum", bufs=CHUNK))
         sum_psum = stack.enter_context(tc.psum_pool(name="sum_psum", bufs=CHUNK))
 
-        def load_motion(b):
-            nc.sync.dma_start(out=m_rows[:, b, :], in_=m[b, :, :])
-
-        def load_query(c):
-            nc.sync.dma_start(
-                out=q_chunks[c][:], in_=query[:, c * CHUNK : (c + 1) * CHUNK, :]
-            )
-
-        m_rows = keep.tile([P, BATCH, FEATURES], BF16)
+        identity_f32 = keep.tile([P, P], F32)
+        m_turned = keep.tile([P, BATCH, WORDS], F32)
+        w_codes = keep.tile([P, PASSES * OUTPUTS], U32, align_bytes=64)
+        w_scales = keep.tile([P, PASSES * OUTPUTS], U8, align_bytes=64)
+        bias_along_free = keep.tile([P, OUTPUTS], F32)
+        bias_by_partition = keep.tile([P, COLUMN_TILES], F32)
         q_chunks = []
         for c in range(N_CHUNKS):
             q_rows = q_pool.tile([P, CHUNK, FEATURES], BF16)
             q_chunks.append(q_rows)
-        load_motion(0)
-        for c in range(LEAD):
-            load_query(c)
-        b_rows = keep.tile([P, COLUMN_TILES, RANK], BF16)
-        nc.sync.dma_start(out=b_rows[:], in_=B_q.rearrange("(h e) r -> e h r", e=P))
-        a_rows = keep.tile([P, FEATURES], BF16)
-        nc.sync.dma_start(out=a_rows[:], in_=A_q)
-        w_rows = keep.tile([P, COLUMN_TILES, FEATURES], BF16)
-        nc.sync.dma_start(out=w_rows[:], in_=w_q.rearrange("(h e) k -> e h k", e=P))
-        bias_row = keep.tile([P, OUTPUTS], BF16)
-        nc.vector.memset(bias_row[:], 0.0)
-        nc.sync.dma_start(out=bias_row[0:1, :], in_=b_q.rearrange("(o e) -> o e", o=1))
-        load_query(LEAD)
-        for b in range(1, BATCH):
-            load_motion(b)
-        for c in range(LEAD + 1, N_CHUNKS):
-            load_query(c)
-
-        identity_f32 = keep.tile([P, P], F32)
-        make_identity(nc, identity_f32[:])
-        identity_bf16 = keep.tile([P, P], BF16)
-        make_identity(nc, identity_bf16[:])
-        ones = keep.tile([P, P], BF16)
-        nc.vector.memset(ones[:], 1.0)
-
-        m_turned = keep.tile([P, BATCH, WORDS], F32)
-
-        def turn_motion(b):
-            bank = turn_psum.tile([P, WORDS], F32, tag="turn")
-            turn_rows(nc, bank, m_rows[:, b, :].bitcast(F32), identity_f32[:])
-            nc.scalar.copy(
-                out=m_turned[:, b, :].rearrange("p (x u) -> p x u", u=HALVES),
-                in_=bank[:].rearrange("p (u x) -> p x u", u=HALVES),
-            )
 
         def turn(c):
             banks = []
@@ -134,17 +99,137 @@ def tile_inversiontemporalmha_pa_t_kernel(tc, query, m, w_q, b_q, A_q, B_q, out)
             )
             return codes, scales
 
-        def multiply(codes, scales):
+        packed = []
+
+        with tc.tile_pool(name="build", bufs=1) as build:
+            def load_motion(b):
+                nc.sync.dma_start(out=m_rows[:, b, :], in_=m[b, :, :])
+
+            def load_query(c):
+                nc.sync.dma_start(
+                    out=q_chunks[c][:], in_=query[:, c * CHUNK : (c + 1) * CHUNK, :]
+                )
+
+            m_rows = build.tile([P, BATCH, FEATURES], BF16)
+            load_motion(0)
+            for c in range(LEAD):
+                load_query(c)
+            b_rows = build.tile([P, COLUMN_TILES, RANK], BF16)
+            nc.sync.dma_start(out=b_rows[:], in_=B_q.rearrange("(h e) r -> e h r", e=P))
+            a_rows = build.tile([P, FEATURES], BF16)
+            nc.sync.dma_start(out=a_rows[:], in_=A_q)
+            w_rows = build.tile([P, COLUMN_TILES, FEATURES], BF16)
+            nc.sync.dma_start(out=w_rows[:], in_=w_q.rearrange("(h e) k -> e h k", e=P))
+            bias_row = build.tile([P, OUTPUTS], BF16)
+            nc.vector.memset(bias_row[:], 0.0)
+            nc.sync.dma_start(out=bias_row[0:1, :], in_=b_q.rearrange("(o e) -> o e", o=1))
+            load_query(LEAD)
+            for b in range(1, BATCH):
+                load_motion(b)
+            for c in range(LEAD + 1, N_CHUNKS):
+                load_query(c)
+
+            make_identity(nc, identity_f32[:])
+            identity_bf16 = build.tile([P, P], BF16)
+            make_identity(nc, identity_bf16[:])
+            ones = build.tile([P, P], BF16)
+            nc.vector.memset(ones[:], 1.0)
+
+            def turn_motion(b):
+                bank = turn_psum.tile([P, WORDS], F32, tag="turn")
+                turn_rows(nc, bank, m_rows[:, b, :].bitcast(F32), identity_f32[:])
+                nc.scalar.copy(
+                    out=m_turned[:, b, :].rearrange("p (x u) -> p x u", u=HALVES),
+                    in_=bank[:].rearrange("p (u x) -> p x u", u=HALVES),
+                )
+
+            turn_motion(0)
+            for c in range(LEAD):
+                packed.append(quantise(add_motion(c, turn(c))))
+
+            b_turned_psum = turn_psum.tile([P, OUTPUTS], BF16, tag="turn")
+            for h in range(COLUMN_TILES):
+                nc.tensor.transpose(
+                    b_turned_psum[:, h * P : (h + 1) * P], b_rows[:, h, :], identity_bf16[:]
+                )
+            b_turned = build.tile([P, OUTPUTS], BF16)
+            nc.scalar.mul(out=b_turned[:], in_=b_turned_psum[:], mul=LORA_SCALE)
+
+            w_grouped = build.tile([P, PASSES, OUTPUTS, PACK], BF16, align_bytes=64)
+            feature_order = "r (g u p e) -> r g u e p"
+            a_by_word = a_rows[:].rearrange(feature_order, g=PASSES, u=HALVES, e=2)
+            for g in range(PASSES):
+                for h in range(COLUMN_TILES):
+                    w_by_word = w_rows[:, h, :].rearrange(feature_order, g=PASSES, u=HALVES, e=2)
+                    w_turned = sum_psum.tile([P, PACK * P], F32, tag="sum")
+                    for u in range(HALVES):
+                        for e in range(2):
+                            plane = w_turned[:, (2 * u + e) * P : (2 * u + e + 1) * P]
+                            nc.tensor.matmul(
+                                out=plane,
+                                lhsT=a_by_word[:, g, u, e, :],
+                                rhs=b_turned[:, h * P : (h + 1) * P],
+                                start=True,
+                                stop=False,
+                            )
+                            nc.tensor.matmul(
+                                out=plane,
+                                lhsT=w_by_word[:, g, u, e, :],
+                                rhs=identity_bf16[:],
+                                start=False,
+                                stop=True,
+                            )
+                    nc.scalar.copy(
+                        out=w_grouped[:, g, h * P : (h + 1) * P, :],
+                        in_=w_turned[:].rearrange("p (j e) -> p e j", j=PACK),
+                    )
+                outputs = slice(g * OUTPUTS, (g + 1) * OUTPUTS)
+                nc.vector.quantize_mx(
+                    out=w_codes[:, outputs].bitcast(FP8X4),
+                    scales=w_scales[:, outputs],
+                    in_=w_grouped[:, g, :, :].rearrange("p e j -> p (e j)"),
+                )
+
+            bias_psum = sum_psum.tile([P, OUTPUTS], F32, tag="sum")
+            nc.tensor.matmul(
+                out=bias_psum[:], lhsT=ones[:], rhs=bias_row[:], start=True, stop=True
+            )
+            nc.scalar.copy(out=bias_along_free[:], in_=bias_psum[:])
+            bias_blocks_psum = sum_psum.tile([P, COLUMN_TILES, P], F32, tag="sum")
+            for h in range(COLUMN_TILES):
+                nc.tensor.matmul(
+                    out=bias_blocks_psum[:, h, :],
+                    lhsT=bias_row[:, h * P : (h + 1) * P],
+                    rhs=ones[:],
+                    start=True,
+                    stop=True,
+                )
+            nc.scalar.copy(out=bias_by_partition[:], in_=bias_blocks_psum[:, :, 0])
+
+            for b in range(1, BATCH):
+                turn_motion(b)
+
+        result_pool = stack.enter_context(tc.tile_pool(name="result", bufs=6))
+        biased_pool = stack.enter_context(tc.tile_pool(name="biased", bufs=2 * TURNED))
+
+        def frame_columns(i, g):
+            return slice((i * PASSES + g) * FRAMES, (i * PASSES + g + 1) * FRAMES)
+
+        def store(c, first, count, result):
+            bj = c * CHUNK + first
+            nc.sync.dma_start(out=out[:, bj : bj + count, :], in_=result[:, 0:count, :])
+
+        def multiply(c, first, count):
+            codes, scales = packed[c]
             sums = []
-            for i in range(CHUNK):
+            for i in range(first, first + count):
                 acc = sum_psum.tile([P, OUTPUTS], F32, tag="sum")
                 for g in range(PASSES):
-                    frames = slice((i * PASSES + g) * FRAMES, (i * PASSES + g + 1) * FRAMES)
                     outputs = slice(g * OUTPUTS, (g + 1) * OUTPUTS)
                     nc.tensor.matmul_mx(
                         out=acc[:],
-                        lhsT=codes[:, frames].bitcast(FP8X4),
-                        lhsT_scale=scales[:, frames],
+                        lhsT=codes[:, frame_columns(i, g)].bitcast(FP8X4),
+                        lhsT_scale=scales[:, frame_columns(i, g)],
                         rhs=w_codes[:, outputs].bitcast(FP8X4),
                         rhs_scale=w_scales[:, outputs],
                         start=(g == 0),
@@ -153,91 +238,72 @@ def tile_inversiontemporalmha_pa_t_kernel(tc, query, m, w_q, b_q, A_q, B_q, out)
                 sums.append(acc)
             return sums
 
-        def finish(c, sums):
-            result = result_pool.tile([P, CHUNK, OUTPUTS], F32)
-            step = 1 if c == N_CHUNKS - 1 else CHUNK
-            for i in range(CHUNK):
-                if i < DETOUR:
-                    nc.scalar.copy(out=result[:, i, :], in_=sums[i][:])
+        def add_bias_and_store(c, first, sums):
+            result = result_pool.tile([P, DIRECT, OUTPUTS], F32)
+            for n in range(len(sums)):
+                if first + n < DETOUR:
+                    nc.scalar.copy(out=result[:, n, :], in_=sums[n][:])
                     nc.gpsimd.tensor_tensor(
-                        out=result[:, i, :], in0=result[:, i, :], in1=bias[:], op=ADD
+                        out=result[:, n, :], in0=result[:, n, :], in1=bias_along_free[:], op=ADD
                     )
                 else:
                     nc.vector.tensor_tensor(
-                        out=result[:, i, :], in0=sums[i][:], in1=bias[:], op=ADD
+                        out=result[:, n, :], in0=sums[n][:], in1=bias_along_free[:], op=ADD
                     )
-                if (i + 1) % step == 0:
-                    done = slice(i + 1 - step, i + 1)
-                    nc.sync.dma_start(
-                        out=out[:, c * CHUNK + i + 1 - step : c * CHUNK + i + 1, :],
-                        in_=result[:, done, :],
+            store(c, first, len(sums), result)
+
+        def multiply_turned(c, first, count):
+            codes, scales = packed[c]
+            turned = []
+            for i in range(first, first + count):
+                acc = sum_psum.tile([P, COLUMN_TILES, FRAMES], F32, tag="sum")
+                biased = biased_pool.tile([P, COLUMN_TILES, FRAMES], F32)
+                for h in range(COLUMN_TILES):
+                    for g in range(PASSES):
+                        outputs = slice(g * OUTPUTS + h * P, g * OUTPUTS + (h + 1) * P)
+                        nc.tensor.matmul_mx(
+                            out=acc[:, h, :],
+                            lhsT=w_codes[:, outputs].bitcast(FP8X4),
+                            lhsT_scale=w_scales[:, outputs],
+                            rhs=codes[:, frame_columns(i, g)].bitcast(FP8X4),
+                            rhs_scale=scales[:, frame_columns(i, g)],
+                            start=(g == 0),
+                            stop=(g == PASSES - 1),
+                        )
+                for h in range(COLUMN_TILES):
+                    nc.scalar.activation(
+                        out=biased[:, h, :],
+                        in_=acc[:, h, :],
+                        func=IDENTITY,
+                        bias=bias_by_partition[:, h : h + 1],
                     )
+                turned.append(biased)
+            return turned
 
-        turn_motion(0)
-        packed = []
-        for c in range(LEAD):
-            packed.append(quantise(add_motion(c, turn(c))))
+        def turn_back_and_store(c, first, turned):
+            result = result_pool.tile([P, DIRECT, OUTPUTS], F32)
+            for n in range(len(turned)):
+                bank = sum_psum.tile([P, COLUMN_TILES, P], F32, tag="sum")
+                for h in range(COLUMN_TILES):
+                    nc.tensor.transpose(bank[:, h, :], turned[n][:, h, :], identity_f32[:])
+                nc.scalar.copy(out=result[:, n, :], in_=bank[:].rearrange("p h e -> p (h e)"))
+            store(c, first, len(turned), result)
 
-        b_turned_psum = turn_psum.tile([P, OUTPUTS], BF16, tag="turn")
-        for h in range(COLUMN_TILES):
-            nc.tensor.transpose(
-                b_turned_psum[:, h * P : (h + 1) * P], b_rows[:, h, :], identity_bf16[:]
-            )
-        b_turned = keep.tile([P, OUTPUTS], BF16)
-        nc.scalar.mul(out=b_turned[:], in_=b_turned_psum[:], mul=LORA_SCALE)
-
-        w_grouped = keep.tile([P, PASSES, OUTPUTS, PACK], BF16, align_bytes=64)
-        w_codes = keep.tile([P, PASSES * OUTPUTS], U32, align_bytes=64)
-        w_scales = keep.tile([P, PASSES * OUTPUTS], U8, align_bytes=64)
-        feature_order = "r (g u p e) -> r g u e p"
-        a_by_word = a_rows[:].rearrange(feature_order, g=PASSES, u=HALVES, e=2)
-        for g in range(PASSES):
-            for h in range(COLUMN_TILES):
-                w_by_word = w_rows[:, h, :].rearrange(feature_order, g=PASSES, u=HALVES, e=2)
-                w_turned = sum_psum.tile([P, PACK * P], F32, tag="sum")
-                for u in range(HALVES):
-                    for e in range(2):
-                        plane = w_turned[:, (2 * u + e) * P : (2 * u + e + 1) * P]
-                        nc.tensor.matmul(
-                            out=plane,
-                            lhsT=a_by_word[:, g, u, e, :],
-                            rhs=b_turned[:, h * P : (h + 1) * P],
-                            start=True,
-                            stop=False,
-                        )
-                        nc.tensor.matmul(
-                            out=plane,
-                            lhsT=w_by_word[:, g, u, e, :],
-                            rhs=identity_bf16[:],
-                            start=False,
-                            stop=True,
-                        )
-                nc.scalar.copy(
-                    out=w_grouped[:, g, h * P : (h + 1) * P, :],
-                    in_=w_turned[:].rearrange("p (j e) -> p e j", j=PACK),
-                )
-            outputs = slice(g * OUTPUTS, (g + 1) * OUTPUTS)
-            nc.vector.quantize_mx(
-                out=w_codes[:, outputs].bitcast(FP8X4),
-                scales=w_scales[:, outputs],
-                in_=w_grouped[:, g, :, :].rearrange("p e j -> p (e j)"),
-            )
-
-        bias_psum = sum_psum.tile([P, OUTPUTS], F32, tag="sum")
-        nc.tensor.matmul(out=bias_psum[:], lhsT=ones[:], rhs=bias_row[:], start=True, stop=True)
-        bias = keep.tile([P, OUTPUTS], F32)
-        nc.scalar.copy(out=bias[:], in_=bias_psum[:])
-
-        for b in range(1, BATCH):
-            turn_motion(b)
-
+        turned = []
         for c in range(N_CHUNKS):
             ahead = c + LEAD
-            if ahead < N_CHUNKS:
+            preparing = ahead < N_CHUNKS
+            if preparing:
                 banks = turn(ahead)
-            sums = multiply(packed[c][0], packed[c][1])
-            if ahead < N_CHUNKS:
+            if turned:
+                turn_back_and_store(c - 1, DIRECT, turned)
+            sums = multiply(c, 0, DIRECT)
+            if preparing:
+                turned = multiply_turned(c, DIRECT, TURNED)
                 grouped = add_motion(ahead, banks)
-            finish(c, sums)
-            if ahead < N_CHUNKS:
+                add_bias_and_store(c, 0, sums)
                 packed.append(quantise(grouped))
+            else:
+                turned = []
+                add_bias_and_store(c, 0, sums)
+                add_bias_and_store(c, DIRECT, multiply(c, DIRECT, TURNED))

@@ -9,7 +9,6 @@ U32 = mybir.dt.uint32
 U8 = mybir.dt.uint8
 FP8X4 = mybir.dt.float8_e4m3fn_x4
 ADD = mybir.AluOpType.add
-IDENTITY = mybir.ActivationFunctionType.Identity
 
 P = 128
 FRAMES = 128
@@ -24,16 +23,15 @@ LORA_SCALE = 2.0
 PACK = 4
 PASSES = FEATURES // (P * PACK)
 WORDS = FEATURES // 2
+PAIR = 2
 HALVES = 2
-COLUMN_TILES = OUTPUTS // P
+OUTPUT_BLOCKS = OUTPUTS // P
 
 CHUNK = 4
 N_CHUNKS = ROWS // CHUNK
 CHUNKS_PER_BATCH = JOINTS // CHUNK
-TURNED = 1
-DIRECT = CHUNK - TURNED
+LEAD = 3
 DETOUR = 1
-LEAD = 2
 
 FLOPS = 2 * FRAMES * ROWS * FEATURES * OUTPUTS + 2 * OUTPUTS * RANK * FEATURES
 
@@ -62,8 +60,7 @@ def tile_inversiontemporalmha_pa_t_kernel(tc, query, m, w_q, b_q, A_q, B_q, out)
         m_turned = keep.tile([P, BATCH, WORDS], F32)
         w_codes = keep.tile([P, PASSES * OUTPUTS], U32, align_bytes=64)
         w_scales = keep.tile([P, PASSES * OUTPUTS], U8, align_bytes=64)
-        bias_along_free = keep.tile([P, OUTPUTS], F32)
-        bias_by_partition = keep.tile([P, COLUMN_TILES], F32)
+        bias = keep.tile([P, OUTPUTS], F32)
         q_chunks = []
         for c in range(N_CHUNKS):
             q_rows = q_pool.tile([P, CHUNK, FEATURES], BF16)
@@ -82,9 +79,9 @@ def tile_inversiontemporalmha_pa_t_kernel(tc, query, m, w_q, b_q, A_q, B_q, out)
             grouped = grouped_pool.tile([P, CHUNK, FEATURES], BF16, align_bytes=64)
             for i in range(CHUNK):
                 nc.vector.tensor_tensor(
-                    out=grouped[:, i, :].rearrange("p (x u e) -> p x u e", u=HALVES, e=2),
-                    in0=banks[i][:].bitcast(BF16).rearrange("p (u x e) -> p x u e", u=HALVES, e=2),
-                    in1=m_turned[:, b, :].bitcast(BF16).rearrange("p (x u e) -> p x u e", u=HALVES, e=2),
+                    out=grouped[:, i, :].rearrange("p (x u e) -> p x u e", u=HALVES, e=PAIR),
+                    in0=banks[i][:].bitcast(BF16).rearrange("p (u x e) -> p x u e", u=HALVES, e=PAIR),
+                    in1=m_turned[:, b, :].bitcast(BF16).rearrange("p (x u e) -> p x u e", u=HALVES, e=PAIR),
                     op=ADD,
                 )
             return grouped
@@ -105,29 +102,33 @@ def tile_inversiontemporalmha_pa_t_kernel(tc, query, m, w_q, b_q, A_q, B_q, out)
             def load_motion(b):
                 nc.sync.dma_start(out=m_rows[:, b, :], in_=m[b, :, :])
 
-            def load_query(c):
-                nc.sync.dma_start(
-                    out=q_chunks[c][:], in_=query[:, c * CHUNK : (c + 1) * CHUNK, :]
-                )
+            def load_query(c, step):
+                for i in range(0, CHUNK, step):
+                    nc.sync.dma_start(
+                        out=q_chunks[c][:, i : i + step, :],
+                        in_=query[:, c * CHUNK + i : c * CHUNK + i + step, :],
+                    )
 
             m_rows = build.tile([P, BATCH, FEATURES], BF16)
             load_motion(0)
-            for c in range(LEAD):
-                load_query(c)
-            b_rows = build.tile([P, COLUMN_TILES, RANK], BF16)
-            nc.sync.dma_start(out=b_rows[:], in_=B_q.rearrange("(h e) r -> e h r", e=P))
+            load_query(0, 1)
+            for c in range(1, LEAD - 1):
+                load_query(c, CHUNK)
+            b_rows = build.tile([P, OUTPUT_BLOCKS, RANK], BF16)
+            nc.sync.dma_start(out=b_rows[:], in_=B_q.rearrange("(h o) r -> o h r", o=P))
             a_rows = build.tile([P, FEATURES], BF16)
             nc.sync.dma_start(out=a_rows[:], in_=A_q)
-            w_rows = build.tile([P, COLUMN_TILES, FEATURES], BF16)
-            nc.sync.dma_start(out=w_rows[:], in_=w_q.rearrange("(h e) k -> e h k", e=P))
+            w_rows = build.tile([P, OUTPUT_BLOCKS, FEATURES], BF16)
+            nc.sync.dma_start(out=w_rows[:], in_=w_q.rearrange("(h o) k -> o h k", o=P))
             bias_row = build.tile([P, OUTPUTS], BF16)
             nc.vector.memset(bias_row[:], 0.0)
-            nc.sync.dma_start(out=bias_row[0:1, :], in_=b_q.rearrange("(o e) -> o e", o=1))
-            load_query(LEAD)
+            nc.sync.dma_start(out=bias_row[0:1, :], in_=b_q.rearrange("(one o) -> one o", one=1))
+            for c in range(LEAD - 1, CHUNKS_PER_BATCH):
+                load_query(c, CHUNK)
             for b in range(1, BATCH):
                 load_motion(b)
-            for c in range(LEAD + 1, N_CHUNKS):
-                load_query(c)
+            for c in range(CHUNKS_PER_BATCH, N_CHUNKS):
+                load_query(c, CHUNK)
 
             make_identity(nc, identity_f32[:])
             identity_bf16 = build.tile([P, P], BF16)
@@ -143,28 +144,22 @@ def tile_inversiontemporalmha_pa_t_kernel(tc, query, m, w_q, b_q, A_q, B_q, out)
                     in_=bank[:].rearrange("p (u x) -> p x u", u=HALVES),
                 )
 
-            turn_motion(0)
-            for c in range(LEAD):
+            def prepare(c):
                 packed.append(quantise(add_motion(c, turn(c))))
 
-            b_turned_psum = turn_psum.tile([P, OUTPUTS], BF16, tag="turn")
-            for h in range(COLUMN_TILES):
-                nc.tensor.transpose(
-                    b_turned_psum[:, h * P : (h + 1) * P], b_rows[:, h, :], identity_bf16[:]
-                )
-            b_turned = build.tile([P, OUTPUTS], BF16)
-            nc.scalar.mul(out=b_turned[:], in_=b_turned_psum[:], mul=LORA_SCALE)
-
             w_grouped = build.tile([P, PASSES, OUTPUTS, PACK], BF16, align_bytes=64)
+            b_turned = build.tile([P, OUTPUTS], BF16)
             feature_order = "r (g u p e) -> r g u e p"
-            a_by_word = a_rows[:].rearrange(feature_order, g=PASSES, u=HALVES, e=2)
-            for g in range(PASSES):
-                for h in range(COLUMN_TILES):
-                    w_by_word = w_rows[:, h, :].rearrange(feature_order, g=PASSES, u=HALVES, e=2)
+
+            def build_w(g):
+                a_by_word = a_rows[:].rearrange(feature_order, g=PASSES, u=HALVES, e=PAIR)
+                for h in range(OUTPUT_BLOCKS):
+                    w_by_word = w_rows[:, h, :].rearrange(feature_order, g=PASSES, u=HALVES, e=PAIR)
                     w_turned = sum_psum.tile([P, PACK * P], F32, tag="sum")
                     for u in range(HALVES):
-                        for e in range(2):
-                            plane = w_turned[:, (2 * u + e) * P : (2 * u + e + 1) * P]
+                        for e in range(PAIR):
+                            j = PAIR * u + e
+                            plane = w_turned[:, j * P : (j + 1) * P]
                             nc.tensor.matmul(
                                 out=plane,
                                 lhsT=a_by_word[:, g, u, e, :],
@@ -181,55 +176,51 @@ def tile_inversiontemporalmha_pa_t_kernel(tc, query, m, w_q, b_q, A_q, B_q, out)
                             )
                     nc.scalar.copy(
                         out=w_grouped[:, g, h * P : (h + 1) * P, :],
-                        in_=w_turned[:].rearrange("p (j e) -> p e j", j=PACK),
+                        in_=w_turned[:].rearrange("p (j o) -> p o j", j=PACK),
                     )
                 outputs = slice(g * OUTPUTS, (g + 1) * OUTPUTS)
                 nc.vector.quantize_mx(
                     out=w_codes[:, outputs].bitcast(FP8X4),
                     scales=w_scales[:, outputs],
-                    in_=w_grouped[:, g, :, :].rearrange("p e j -> p (e j)"),
+                    in_=w_grouped[:, g, :, :].rearrange("p o j -> p (o j)"),
                 )
+
+            turn_motion(0)
+            for c in range(LEAD - 1):
+                prepare(c)
+            b_turned_psum = turn_psum.tile([P, OUTPUTS], BF16, tag="turn")
+            for h in range(OUTPUT_BLOCKS):
+                nc.tensor.transpose(
+                    b_turned_psum[:, h * P : (h + 1) * P], b_rows[:, h, :], identity_bf16[:]
+                )
+            nc.scalar.mul(out=b_turned[:], in_=b_turned_psum[:], mul=LORA_SCALE)
+            build_w(0)
+            prepare(LEAD - 1)
+            build_w(1)
 
             bias_psum = sum_psum.tile([P, OUTPUTS], F32, tag="sum")
             nc.tensor.matmul(
                 out=bias_psum[:], lhsT=ones[:], rhs=bias_row[:], start=True, stop=True
             )
-            nc.scalar.copy(out=bias_along_free[:], in_=bias_psum[:])
-            bias_blocks_psum = sum_psum.tile([P, COLUMN_TILES, P], F32, tag="sum")
-            for h in range(COLUMN_TILES):
-                nc.tensor.matmul(
-                    out=bias_blocks_psum[:, h, :],
-                    lhsT=bias_row[:, h * P : (h + 1) * P],
-                    rhs=ones[:],
-                    start=True,
-                    stop=True,
-                )
-            nc.scalar.copy(out=bias_by_partition[:], in_=bias_blocks_psum[:, :, 0])
+            nc.scalar.copy(out=bias[:], in_=bias_psum[:])
 
             for b in range(1, BATCH):
                 turn_motion(b)
 
-        result_pool = stack.enter_context(tc.tile_pool(name="result", bufs=6))
-        biased_pool = stack.enter_context(tc.tile_pool(name="biased", bufs=2 * TURNED))
+        result_pool = stack.enter_context(tc.tile_pool(name="result", bufs=3))
 
-        def frame_columns(i, g):
-            return slice((i * PASSES + g) * FRAMES, (i * PASSES + g + 1) * FRAMES)
-
-        def store(c, first, count, result):
-            bj = c * CHUNK + first
-            nc.sync.dma_start(out=out[:, bj : bj + count, :], in_=result[:, 0:count, :])
-
-        def multiply(c, first, count):
+        def multiply(c):
             codes, scales = packed[c]
             sums = []
-            for i in range(first, first + count):
+            for i in range(CHUNK):
                 acc = sum_psum.tile([P, OUTPUTS], F32, tag="sum")
                 for g in range(PASSES):
+                    frames = slice((i * PASSES + g) * FRAMES, (i * PASSES + g + 1) * FRAMES)
                     outputs = slice(g * OUTPUTS, (g + 1) * OUTPUTS)
                     nc.tensor.matmul_mx(
                         out=acc[:],
-                        lhsT=codes[:, frame_columns(i, g)].bitcast(FP8X4),
-                        lhsT_scale=scales[:, frame_columns(i, g)],
+                        lhsT=codes[:, frames].bitcast(FP8X4),
+                        lhsT_scale=scales[:, frames],
                         rhs=w_codes[:, outputs].bitcast(FP8X4),
                         rhs_scale=w_scales[:, outputs],
                         start=(g == 0),
@@ -238,72 +229,32 @@ def tile_inversiontemporalmha_pa_t_kernel(tc, query, m, w_q, b_q, A_q, B_q, out)
                 sums.append(acc)
             return sums
 
-        def add_bias_and_store(c, first, sums):
-            result = result_pool.tile([P, DIRECT, OUTPUTS], F32)
-            for n in range(len(sums)):
-                if first + n < DETOUR:
-                    nc.scalar.copy(out=result[:, n, :], in_=sums[n][:])
+        def finish(c, sums):
+            result = result_pool.tile([P, CHUNK, OUTPUTS], F32)
+            step = 1 if c == N_CHUNKS - 1 else CHUNK
+            for i in range(CHUNK):
+                if i < DETOUR:
+                    nc.scalar.copy(out=result[:, i, :], in_=sums[i][:])
                     nc.gpsimd.tensor_tensor(
-                        out=result[:, n, :], in0=result[:, n, :], in1=bias_along_free[:], op=ADD
+                        out=result[:, i, :], in0=result[:, i, :], in1=bias[:], op=ADD
                     )
                 else:
                     nc.vector.tensor_tensor(
-                        out=result[:, n, :], in0=sums[n][:], in1=bias_along_free[:], op=ADD
+                        out=result[:, i, :], in0=sums[i][:], in1=bias[:], op=ADD
                     )
-            store(c, first, len(sums), result)
-
-        def multiply_turned(c, first, count):
-            codes, scales = packed[c]
-            turned = []
-            for i in range(first, first + count):
-                acc = sum_psum.tile([P, COLUMN_TILES, FRAMES], F32, tag="sum")
-                biased = biased_pool.tile([P, COLUMN_TILES, FRAMES], F32)
-                for h in range(COLUMN_TILES):
-                    for g in range(PASSES):
-                        outputs = slice(g * OUTPUTS + h * P, g * OUTPUTS + (h + 1) * P)
-                        nc.tensor.matmul_mx(
-                            out=acc[:, h, :],
-                            lhsT=w_codes[:, outputs].bitcast(FP8X4),
-                            lhsT_scale=w_scales[:, outputs],
-                            rhs=codes[:, frame_columns(i, g)].bitcast(FP8X4),
-                            rhs_scale=scales[:, frame_columns(i, g)],
-                            start=(g == 0),
-                            stop=(g == PASSES - 1),
-                        )
-                for h in range(COLUMN_TILES):
-                    nc.scalar.activation(
-                        out=biased[:, h, :],
-                        in_=acc[:, h, :],
-                        func=IDENTITY,
-                        bias=bias_by_partition[:, h : h + 1],
+                if (i + 1) % step == 0:
+                    nc.sync.dma_start(
+                        out=out[:, c * CHUNK + i + 1 - step : c * CHUNK + i + 1, :],
+                        in_=result[:, i + 1 - step : i + 1, :],
                     )
-                turned.append(biased)
-            return turned
 
-        def turn_back_and_store(c, first, turned):
-            result = result_pool.tile([P, DIRECT, OUTPUTS], F32)
-            for n in range(len(turned)):
-                bank = sum_psum.tile([P, COLUMN_TILES, P], F32, tag="sum")
-                for h in range(COLUMN_TILES):
-                    nc.tensor.transpose(bank[:, h, :], turned[n][:, h, :], identity_f32[:])
-                nc.scalar.copy(out=result[:, n, :], in_=bank[:].rearrange("p h e -> p (h e)"))
-            store(c, first, len(turned), result)
-
-        turned = []
         for c in range(N_CHUNKS):
             ahead = c + LEAD
-            preparing = ahead < N_CHUNKS
-            if preparing:
+            if ahead < N_CHUNKS:
                 banks = turn(ahead)
-            if turned:
-                turn_back_and_store(c - 1, DIRECT, turned)
-            sums = multiply(c, 0, DIRECT)
-            if preparing:
-                turned = multiply_turned(c, DIRECT, TURNED)
+            sums = multiply(c)
+            if ahead < N_CHUNKS:
                 grouped = add_motion(ahead, banks)
-                add_bias_and_store(c, 0, sums)
+            finish(c, sums)
+            if ahead < N_CHUNKS:
                 packed.append(quantise(grouped))
-            else:
-                turned = []
-                add_bias_and_store(c, 0, sums)
-                add_bias_and_store(c, DIRECT, multiply(c, DIRECT, TURNED))

from contextlib import ExitStack

import concourse.mybir as mybir
from concourse.masks import make_identity

BF16 = mybir.dt.bfloat16
F32 = mybir.dt.float32
U32 = mybir.dt.uint32
U8 = mybir.dt.uint8
FP8X4 = mybir.dt.float8_e4m3fn_x4
ADD = mybir.AluOpType.add

P = 128
FRAMES = 128
BATCH = 4
JOINTS = 16
ROWS = BATCH * JOINTS
FEATURES = 1024
OUTPUTS = 512
RANK = 128
LORA_SCALE = 2.0

PACK = 4
PASSES = FEATURES // (P * PACK)
WORDS = FEATURES // 2
PAIR = 2
HALVES = 2
OUTPUT_BLOCKS = OUTPUTS // P

CHUNK = 4
N_CHUNKS = ROWS // CHUNK
CHUNKS_PER_BATCH = JOINTS // CHUNK
LEAD = 3
DETOUR = 1

FLOPS = 2 * FRAMES * ROWS * FEATURES * OUTPUTS + 2 * OUTPUTS * RANK * FEATURES


def turn_rows(nc, bank, row_words, identity):
    for u in range(HALVES):
        for g in range(PASSES):
            nc.tensor.transpose(
                bank[:, (u * PASSES + g) * P : (u * PASSES + g + 1) * P],
                row_words[:, (g * HALVES + u) * P : (g * HALVES + u + 1) * P],
                identity,
            )


def tile_inversiontemporalmha_pa_t_kernel(tc, query, m, w_q, b_q, A_q, B_q, out):
    nc = tc.nc
    with ExitStack() as stack:
        keep = stack.enter_context(tc.tile_pool(name="keep", bufs=1))
        q_pool = stack.enter_context(tc.tile_pool(name="q", bufs=N_CHUNKS))
        grouped_pool = stack.enter_context(tc.tile_pool(name="grouped", bufs=2))
        packed_pool = stack.enter_context(tc.tile_pool(name="packed", bufs=LEAD + 1))
        turn_psum = stack.enter_context(tc.psum_pool(name="turn_psum", bufs=CHUNK))
        sum_psum = stack.enter_context(tc.psum_pool(name="sum_psum", bufs=CHUNK))

        identity_f32 = keep.tile([P, P], F32)
        m_turned = keep.tile([P, BATCH, WORDS], F32)
        w_codes = keep.tile([P, PASSES * OUTPUTS], U32, align_bytes=64)
        w_scales = keep.tile([P, PASSES * OUTPUTS], U8, align_bytes=64)
        bias = keep.tile([P, OUTPUTS], F32)
        q_chunks = []
        for c in range(N_CHUNKS):
            q_rows = q_pool.tile([P, CHUNK, FEATURES], BF16)
            q_chunks.append(q_rows)

        def turn(c):
            banks = []
            for i in range(CHUNK):
                bank = turn_psum.tile([P, WORDS], F32, tag="turn")
                turn_rows(nc, bank, q_chunks[c][:, i, :].bitcast(F32), identity_f32[:])
                banks.append(bank)
            return banks

        def add_motion(c, banks):
            b = c // CHUNKS_PER_BATCH
            grouped = grouped_pool.tile([P, CHUNK, FEATURES], BF16, align_bytes=64)
            for i in range(CHUNK):
                nc.vector.tensor_tensor(
                    out=grouped[:, i, :].rearrange("p (x u e) -> p x u e", u=HALVES, e=PAIR),
                    in0=banks[i][:].bitcast(BF16).rearrange("p (u x e) -> p x u e", u=HALVES, e=PAIR),
                    in1=m_turned[:, b, :].bitcast(BF16).rearrange("p (x u e) -> p x u e", u=HALVES, e=PAIR),
                    op=ADD,
                )
            return grouped

        def quantise(grouped):
            codes = packed_pool.tile([P, CHUNK * PASSES * FRAMES], U32, align_bytes=64)
            scales = packed_pool.tile([P, CHUNK * PASSES * FRAMES], U8, align_bytes=64)
            nc.vector.quantize_mx(
                out=codes[:].bitcast(FP8X4),
                scales=scales[:],
                in_=grouped[:].rearrange("p i n -> p (i n)"),
            )
            return codes, scales

        packed = []

        with tc.tile_pool(name="build", bufs=1) as build:
            def load_motion(b):
                nc.sync.dma_start(out=m_rows[:, b, :], in_=m[b, :, :])

            def load_query(c, step):
                for i in range(0, CHUNK, step):
                    nc.sync.dma_start(
                        out=q_chunks[c][:, i : i + step, :],
                        in_=query[:, c * CHUNK + i : c * CHUNK + i + step, :],
                    )

            m_rows = build.tile([P, BATCH, FEATURES], BF16)
            load_motion(0)
            load_query(0, 1)
            for c in range(1, LEAD - 1):
                load_query(c, CHUNK)
            b_rows = build.tile([P, OUTPUT_BLOCKS, RANK], BF16)
            nc.sync.dma_start(out=b_rows[:], in_=B_q.rearrange("(h o) r -> o h r", o=P))
            a_rows = build.tile([P, FEATURES], BF16)
            nc.sync.dma_start(out=a_rows[:], in_=A_q)
            w_rows = build.tile([P, OUTPUT_BLOCKS, FEATURES], BF16)
            nc.sync.dma_start(out=w_rows[:], in_=w_q.rearrange("(h o) k -> o h k", o=P))
            bias_row = build.tile([P, OUTPUTS], BF16)
            nc.vector.memset(bias_row[:], 0.0)
            nc.sync.dma_start(out=bias_row[0:1, :], in_=b_q.rearrange("(one o) -> one o", one=1))
            for c in range(LEAD - 1, CHUNKS_PER_BATCH):
                load_query(c, CHUNK)
            for b in range(1, BATCH):
                load_motion(b)
            for c in range(CHUNKS_PER_BATCH, N_CHUNKS):
                load_query(c, CHUNK)

            make_identity(nc, identity_f32[:])
            identity_bf16 = build.tile([P, P], BF16)
            make_identity(nc, identity_bf16[:])
            ones = build.tile([P, P], BF16)
            nc.vector.memset(ones[:], 1.0)

            def turn_motion(b):
                bank = turn_psum.tile([P, WORDS], F32, tag="turn")
                turn_rows(nc, bank, m_rows[:, b, :].bitcast(F32), identity_f32[:])
                nc.scalar.copy(
                    out=m_turned[:, b, :].rearrange("p (x u) -> p x u", u=HALVES),
                    in_=bank[:].rearrange("p (u x) -> p x u", u=HALVES),
                )

            def prepare(c):
                packed.append(quantise(add_motion(c, turn(c))))

            w_grouped = build.tile([P, PASSES, OUTPUTS, PACK], BF16, align_bytes=64)
            b_turned = build.tile([P, OUTPUTS], BF16)
            feature_order = "r (g u p e) -> r g u e p"

            def build_w(g):
                a_by_word = a_rows[:].rearrange(feature_order, g=PASSES, u=HALVES, e=PAIR)
                for h in range(OUTPUT_BLOCKS):
                    w_by_word = w_rows[:, h, :].rearrange(feature_order, g=PASSES, u=HALVES, e=PAIR)
                    w_turned = sum_psum.tile([P, PACK * P], F32, tag="sum")
                    for u in range(HALVES):
                        for e in range(PAIR):
                            j = PAIR * u + e
                            plane = w_turned[:, j * P : (j + 1) * P]
                            nc.tensor.matmul(
                                out=plane,
                                lhsT=a_by_word[:, g, u, e, :],
                                rhs=b_turned[:, h * P : (h + 1) * P],
                                start=True,
                                stop=False,
                            )
                            nc.tensor.matmul(
                                out=plane,
                                lhsT=w_by_word[:, g, u, e, :],
                                rhs=identity_bf16[:],
                                start=False,
                                stop=True,
                            )
                    nc.scalar.copy(
                        out=w_grouped[:, g, h * P : (h + 1) * P, :],
                        in_=w_turned[:].rearrange("p (j o) -> p o j", j=PACK),
                    )
                outputs = slice(g * OUTPUTS, (g + 1) * OUTPUTS)
                nc.vector.quantize_mx(
                    out=w_codes[:, outputs].bitcast(FP8X4),
                    scales=w_scales[:, outputs],
                    in_=w_grouped[:, g, :, :].rearrange("p o j -> p (o j)"),
                )

            turn_motion(0)
            for c in range(LEAD - 1):
                prepare(c)
            b_turned_psum = turn_psum.tile([P, OUTPUTS], BF16, tag="turn")
            for h in range(OUTPUT_BLOCKS):
                nc.tensor.transpose(
                    b_turned_psum[:, h * P : (h + 1) * P], b_rows[:, h, :], identity_bf16[:]
                )
            nc.scalar.mul(out=b_turned[:], in_=b_turned_psum[:], mul=LORA_SCALE)
            build_w(0)
            prepare(LEAD - 1)
            build_w(1)

            bias_psum = sum_psum.tile([P, OUTPUTS], F32, tag="sum")
            nc.tensor.matmul(
                out=bias_psum[:], lhsT=ones[:], rhs=bias_row[:], start=True, stop=True
            )
            nc.scalar.copy(out=bias[:], in_=bias_psum[:])

            for b in range(1, BATCH):
                turn_motion(b)

        result_pool = stack.enter_context(tc.tile_pool(name="result", bufs=3))

        def multiply(c):
            codes, scales = packed[c]
            sums = []
            for i in range(CHUNK):
                acc = sum_psum.tile([P, OUTPUTS], F32, tag="sum")
                for g in range(PASSES):
                    frames = slice((i * PASSES + g) * FRAMES, (i * PASSES + g + 1) * FRAMES)
                    outputs = slice(g * OUTPUTS, (g + 1) * OUTPUTS)
                    nc.tensor.matmul_mx(
                        out=acc[:],
                        lhsT=codes[:, frames].bitcast(FP8X4),
                        lhsT_scale=scales[:, frames],
                        rhs=w_codes[:, outputs].bitcast(FP8X4),
                        rhs_scale=w_scales[:, outputs],
                        start=(g == 0),
                        stop=(g == PASSES - 1),
                    )
                sums.append(acc)
            return sums

        def finish(c, sums):
            result = result_pool.tile([P, CHUNK, OUTPUTS], F32)
            step = 1 if c == N_CHUNKS - 1 else CHUNK
            for i in range(CHUNK):
                if i < DETOUR:
                    nc.scalar.copy(out=result[:, i, :], in_=sums[i][:])
                    nc.gpsimd.tensor_tensor(
                        out=result[:, i, :], in0=result[:, i, :], in1=bias[:], op=ADD
                    )
                else:
                    nc.vector.tensor_tensor(
                        out=result[:, i, :], in0=sums[i][:], in1=bias[:], op=ADD
                    )
                if (i + 1) % step == 0:
                    nc.sync.dma_start(
                        out=out[:, c * CHUNK + i + 1 - step : c * CHUNK + i + 1, :],
                        in_=result[:, i + 1 - step : i + 1, :],
                    )

        for c in range(N_CHUNKS):
            ahead = c + LEAD
            if ahead < N_CHUNKS:
                banks = turn(ahead)
            sums = multiply(c)
            if ahead < N_CHUNKS:
                grouped = add_motion(ahead, banks)
            finish(c, sums)
            if ahead < N_CHUNKS:
                packed.append(quantise(grouped))
